import numpy as np
import ml_dtypes


def mxq(x, axis, fmt="e4m3"):
    dtype, down = {"e4m3": (ml_dtypes.float8_e4m3fn, 7), "e5m2": (ml_dtypes.float8_e5m2, 14)}[fmt]
    v = np.moveaxis(np.asarray(x, np.float32).astype(ml_dtypes.bfloat16).astype(np.float64), axis, -1)
    blocks = v.reshape(v.shape[:-1] + (-1, 32))
    amax = np.abs(blocks).max(-1, keepdims=True)
    byte = np.maximum(np.where(amax > 0, np.frexp(amax)[1] - 1 + 127, 0) - down, 1)
    scale = np.exp2(byte - 127.0)
    codes = (blocks / scale).astype(np.float32).astype(dtype).astype(np.float64)
    return np.moveaxis((codes * scale).reshape(v.shape), -1, axis)


BF16 = ml_dtypes.bfloat16


def bf(x):
    return np.asarray(x, np.float32).astype(BF16)


def f64(x):
    return np.asarray(x).astype(np.float64)


B, P, C, H = 1, 8192, 512, 8
WD = P // H
GS = 2.0


def setup_inputs():
    return {"qkv_bn": bf(np.random.standard_normal((B, C, P)) * GS / np.sqrt(np.sqrt(WD))),
            "gra_sharp": bf(GS * (1.0 + 0.1 * np.random.standard_normal(1)))}


def reference(qkv_bn, gra_sharp):
    q = f64(qkv_bn).reshape(B, C, H, WD).transpose(0, 2, 1, 3)
    scores = q @ q.transpose(0, 1, 3, 2) / f64(gra_sharp)
    e = np.exp(scores - scores.max(1, keepdims=True))
    attn = e / e.sum(1, keepdims=True)
    o = mxq(attn, 3, "e4m3") @ mxq(q, 2, "e4m3")
    h = o.transpose(0, 2, 1, 3).reshape(B, C, P).transpose(0, 2, 1)
    return h, attn

@@ -1,0 +1,185 @@
+from contextlib import ExitStack
+
+import concourse.mybir as mybir
+from concourse.masks import make_identity
+
+F32 = mybir.dt.float32
+BF16 = mybir.dt.bfloat16
+U8 = mybir.dt.uint8
+U32 = mybir.dt.uint32
+FP8X4 = mybir.dt.float8_e4m3fn_x4
+ALU = mybir.AluOpType
+ACT = mybir.ActivationFunctionType
+AX = mybir.AxisListType
+
+P = 128
+C = 512
+H = 8
+WD = 1024
+T = C // P
+KIB = 1024
+
+FLOPS = 2 * 2 * H * C * C * WD
+
+
+def tile_channelgroupattention_pa_kernel(tc, qkv_bn, gra_sharp, out_0, out_1):
+    nc = tc.nc
+    x = qkv_bn.rearrange("b c w -> (b c) w")
+    h2 = out_0.rearrange("b w c -> (b w) c")
+    attn3 = out_1.rearrange("b n c d -> (b n) c d")
+
+    with ExitStack() as ctx:
+        big = ctx.enter_context(tc.tile_pool(name="big", bufs=1))
+        const = ctx.enter_context(tc.tile_pool(name="const", bufs=1))
+        small = ctx.enter_context(tc.tile_pool(name="small", bufs=2))
+        dpool = ctx.enter_context(tc.tile_pool(name="dpool", bufs=3))
+        stage = ctx.enter_context(tc.tile_pool(name="stage", bufs=2))
+        psum = ctx.enter_context(tc.psum_pool(name="psum", bufs=4))
+
+        xs = [big.tile([P, T, 2 * WD], BF16, name="x%d" % hp, offset=hp * 16 * KIB, align_bytes=64)
+              for hp in range(4)]
+        qt = [big.tile([P, H, 4, P], F32, name="qt%d" % t, offset=(64 + 16 * t) * KIB, align_bytes=64)
+              for t in range(T)]
+        rng = [big.tile([P, T, H, P], F32, name="rng%d" % j, offset=(128 + 16 * j) * KIB, align_bytes=64)
+               for j in range(T)]
+
+        ident = const.tile([P, P], F32, name="ident")
+        make_identity(nc, ident[:])
+        g_bf = const.tile([P, 1], BF16, name="g_bf")
+        with nc.allow_non_contiguous_dma(reason="one bf16 scalar to every partition"):
+            nc.scalar.dma_start(out=g_bf[:], in_=gra_sharp.partition_broadcast(P))
+        g_f = const.tile([P, 1], F32, name="g_f")
+        nc.vector.tensor_copy(out=g_f[:], in_=g_bf[:])
+        rg = const.tile([P, 1], F32, name="rg")
+        nc.vector.reciprocal(out=rg[:], in_=g_f[:])
+
+        for t in range(T):
+            for hp in range(4):
+                nc.sync.dma_start(out=xs[hp][:, t, :],
+                                  in_=x[P * t:P * (t + 1), 2 * WD * hp:2 * WD * (hp + 1)])
+
+        def x_transposes(t):
+            for n in range(H):
+                tb = psum.tile([P, 4, P], F32, name="tb", tag="tp")
+                base = WD * (n % 2)
+                for u in range(4):
+                    nc.tensor.transpose(
+                        tb[:, u, :],
+                        xs[n // 2][:, t, base + 256 * u:base + 256 * (u + 1)].bitcast(F32),
+                        ident[:])
+                if n % 2 == 1:
+                    nc.vector.tensor_copy(out=qt[t][:, n, :, :], in_=tb[:])
+                else:
+                    nc.scalar.copy(out=qt[t][:, n, :, :], in_=tb[:])
+
+        def qtb(t, n, u, e):
+            return qt[t][:, n, u, :].bitcast(BF16).rearrange("p (c e) -> p c e", e=2)[:, :, e]
+
+        def store_block(a, b):
+            nc.sync.dma_start(
+                out=attn3[:, P * a:P * (a + 1), P * b:P * (b + 1)].rearrange("n p c -> p n c"),
+                in_=rng[b][:, a, :, :])
+
+        def block(i, j):
+            banks = []
+            for hh in range(2):
+                bank = psum.tile([P, 4, P], F32, name="sc", tag="sc")
+                for nn in range(4):
+                    n = 4 * hh + nn
+                    for u in range(4):
+                        for e in range(2):
+                            nc.tensor.matmul(out=bank[:, nn, :], lhsT=qtb(i, n, u, e), rhs=qtb(j, n, u, e),
+                                             start=(u == 0 and e == 0), stop=(u == 3 and e == 1))
+                banks.append(bank)
+            pm = small.tile([P, 2, P], F32, name="pm", tag="pm")
+            for hh in range(2):
+                nc.vector.tensor_reduce(out=pm[:, hh, :], in_=banks[hh][:].rearrange("p h c -> p c h"),
+                                        axis=AX.X, op=ALU.max)
+            m = small.tile([P, P], F32, name="m", tag="m")
+            nc.vector.tensor_tensor(out=m[:], in0=pm[:, 0, :], in1=pm[:, 1, :], op=ALU.max)
+            d = dpool.tile([P, H, P], F32, name="d", tag="d")
+            for hh in range(2):
+                nc.vector.tensor_tensor(out=d[:, 4 * hh:4 * (hh + 1), :], in0=banks[hh][:],
+                                        in1=m[:].unsqueeze(1).to_broadcast([P, 4, P]), op=ALU.subtract)
+            nc.scalar.activation(out=d[:], in_=d[:], func=ACT.Exp, scale=rg[:, 0:1])
+            z = small.tile([P, P], F32, name="z", tag="z")
+            nc.vector.tensor_reduce(out=z[:], in_=d[:].rearrange("p h c -> p c h"), axis=AX.X, op=ALU.add)
+            r = small.tile([P, P], F32, name="r", tag="r")
+            nc.vector.reciprocal(out=r[:], in_=z[:])
+            nc.gpsimd.tensor_tensor(out=rng[j][:, i, :, :], in0=d[:],
+                                    in1=r[:].unsqueeze(1).to_broadcast([P, H, P]), op=ALU.mult)
+            store_block(i, j)
+            if i < j:
+                for hh in range(2):
+                    tb = psum.tile([P, 4, P], F32, name="tb", tag="tp")
+                    for nn in range(4):
+                        nc.tensor.transpose(tb[:, nn, :], rng[j][:, i, 4 * hh + nn, :], ident[:])
+                    nc.scalar.copy(out=rng[i][:, j, 4 * hh:4 * (hh + 1), :], in_=tb[:])
+                store_block(j, i)
+
+        def quantise_range(j, ac, asc, engines):
+            for k in range(4):
+                ga = stage.tile([P, 2, P, 4], BF16, name="ga", tag="ga", bufs=4, align_bytes=64)
+                src = rng[j][:, :, 2 * k:2 * (k + 1), :].rearrange("p t n c -> p n c t")
+                if engines[k] == "v":
+                    nc.vector.tensor_copy(out=ga[:], in_=src)
+                else:
+                    nc.scalar.copy(out=ga[:], in_=src)
+                for nn in range(2):
+                    n = 2 * k + nn
+                    nc.vector.quantize_mx(out=ac[:, n, P * j:P * (j + 1)].bitcast(FP8X4),
+                                          scales=asc[:, n, P * j:P * (j + 1)],
+                                          in_=ga[:, nn, :, :].rearrange("p c t -> p (c t)"))
+
+        for t in range(T):
+            x_transposes(t)
+            block(0, t)
+        for j in range(1, T):
+            block(1, j)
+        ac = big.tile([P, H, C], U32, name="ac", offset=80 * KIB, align_bytes=64)
+        asc = big.tile([P, H, C], U8, name="asc", offset=74 * KIB, align_bytes=64)
+        quantise_range(0, ac, asc, "ssss")
+        quantise_range(1, ac, asc, "ssss")
+        block(2, 2)
+        block(2, 3)
+        quantise_range(2, ac, asc, "ssss")
+        block(3, 3)
+        quantise_range(3, ac, asc, "vsvs")
+
+        qc_off = [64, 0, 16, 32]
+        qc = []
+        qs = []
+        for hp in range(4):
+            qc_t = big.tile([P, 2, WD], U32, name="qc%d" % hp, offset=qc_off[hp] * KIB, align_bytes=64)
+            qs_t = big.tile([P, 2, WD], U8, name="qs%d" % hp, offset=(qc_off[hp] + 8) * KIB, align_bytes=64)
+            qc.append(qc_t)
+            qs.append(qs_t)
+            for hh in range(2):
+                xv = xs[hp][:, :, WD * hh:WD * (hh + 1)].rearrange("p t (m r) -> p r m t", r=8)
+                for a in range(2):
+                    gq = stage.tile([P, 4, P, 4], BF16, name="gq", tag="gq", bufs=2, align_bytes=64)
+                    nc.gpsimd.tensor_scalar(out=gq[:], in0=xv[:, 4 * a:4 * (a + 1), :, :], scalar1=1.0, scalar2=0.0,
+                                            op0=ALU.mult, op1=ALU.add)
+                    nc.vector.quantize_mx(out=qc_t[:, hh, 512 * a:512 * (a + 1)].bitcast(FP8X4),
+                                          scales=qs_t[:, hh, 512 * a:512 * (a + 1)],
+                                          in_=gq[:].rearrange("p r m t -> p (r m t)"))
+
+        h_off = [96, 104, 112, 120, 128, 136, 144, 152, 160, 168, 176, 184, 96, 104, 112, 120]
+        for n in range(H):
+            hv = h2[WD * n:WD * (n + 1), :].rearrange("(m r) c -> m r c", r=8)
+            for a in range(2):
+                hsb = big.tile([P, 4, C], F32, name="h%d_%d" % (n, a), offset=h_off[2 * n + a] * KIB, align_bytes=64)
+                for rr in range(4):
+                    r8 = 4 * a + rr
+                    bank = psum.tile([P, C], F32, name="hb", tag=("tp" if rr % 2 == 0 else "sc"))
+                    nc.tensor.matmul_mx(out=bank[:],
+                                        lhsT=qc[n // 2][:, n % 2, P * r8:P * (r8 + 1)].bitcast(FP8X4),
+                                        lhsT_scale=qs[n // 2][:, n % 2, P * r8:P * (r8 + 1)],
+                                        rhs=ac[:, n, :].bitcast(FP8X4),
+                                        rhs_scale=asc[:, n, :],
+                                        start=True, stop=True)
+                    if rr % 2 == 0:
+                        nc.scalar.copy(out=hsb[:, rr, :], in_=bank[:])
+                    else:
+                        nc.vector.tensor_copy(out=hsb[:, rr, :], in_=bank[:])
+                nc.sync.dma_start(out=hv[:, 4 * a:4 * (a + 1), :], in_=hsb[:])

@@ -21,6 +21,11 @@ KIB = 1024
 
 FLOPS = 2 * 2 * H * C * C * WD
 
+MULT_G = False
+RG_G = False
+BLOCKS = [(0, 0), (0, 1), (0, 2), (0, 3), (1, 1), (1, 2), (1, 3), (2, 2), (2, 3), (3, 3)]
+XLAG = 3
+
 
 def tile_channelgroupattention_pa_kernel(tc, qkv_bn, gra_sharp, out_0, out_1):
     nc = tc.nc
@@ -33,8 +38,9 @@ def tile_channelgroupattention_pa_kernel(tc, qkv_bn, gra_sharp, out_0, out_1):
         const = ctx.enter_context(tc.tile_pool(name="const", bufs=1))
         small = ctx.enter_context(tc.tile_pool(name="small", bufs=2))
         dpool = ctx.enter_context(tc.tile_pool(name="dpool", bufs=3))
-        stage = ctx.enter_context(tc.tile_pool(name="stage", bufs=2))
-        psum = ctx.enter_context(tc.psum_pool(name="psum", bufs=4))
+        stage = ctx.enter_context(tc.tile_pool(name="stage", bufs=4))
+        psum = ctx.enter_context(tc.psum_pool(name="psum", bufs=1))
+        ctx.enter_context(tc.manual_schedule())
 
         xs = [big.tile([P, T, 2 * WD], BF16, name="x%d" % hp, offset=hp * 16 * KIB, align_bytes=64)
               for hp in range(4)]
@@ -52,25 +58,32 @@ def tile_channelgroupattention_pa_kernel(tc, qkv_bn, gra_sharp, out_0, out_1):
         nc.vector.tensor_copy(out=g_f[:], in_=g_bf[:])
         rg = const.tile([P, 1], F32, name="rg")
         nc.vector.reciprocal(out=rg[:], in_=g_f[:])
+        asc = const.tile([P, H, C], U8, name="asc", align_bytes=64)
+        qc01 = const.tile([P, 2, WD], U32, name="qc01", align_bytes=64)
+        qs01 = const.tile([P, 2, WD], U8, name="qs01", align_bytes=64)
 
         for t in range(T):
             for hp in range(4):
                 nc.sync.dma_start(out=xs[hp][:, t, :],
                                   in_=x[P * t:P * (t + 1), 2 * WD * hp:2 * WD * (hp + 1)])
 
-        def x_transposes(t):
-            for n in range(H):
-                tb = psum.tile([P, 4, P], F32, name="tb", tag="tp")
-                base = WD * (n % 2)
-                for u in range(4):
-                    nc.tensor.transpose(
-                        tb[:, u, :],
-                        xs[n // 2][:, t, base + 256 * u:base + 256 * (u + 1)].bitcast(F32),
-                        ident[:])
-                if n % 2 == 1:
-                    nc.vector.tensor_copy(out=qt[t][:, n, :, :], in_=tb[:])
-                else:
-                    nc.scalar.copy(out=qt[t][:, n, :, :], in_=tb[:])
+        def bank(idx):
+            return psum.tile([P, 4, P], F32, name="bk%d" % idx, tag="bk%d" % idx)
+
+        def copy_on(eng, out, in_):
+            if eng == "v":
+                nc.vector.tensor_copy(out=out, in_=in_)
+            else:
+                nc.scalar.copy(out=out, in_=in_)
+
+        def x_transpose_bank(t, n, idx, eng):
+            tb = bank(idx)
+            base = WD * (n % 2)
+            for u in range(4):
+                nc.tensor.transpose(tb[:, u, :],
+                                    xs[n // 2][:, t, base + 256 * u:base + 256 * (u + 1)].bitcast(F32),
+                                    ident[:])
+            copy_on(eng, qt[t][:, n, :, :], tb[:])
 
         def qtb(t, n, u, e):
             return qt[t][:, n, u, :].bitcast(BF16).rearrange("p (c e) -> p c e", e=2)[:, :, e]
@@ -80,106 +93,187 @@ def tile_channelgroupattention_pa_kernel(tc, qkv_bn, gra_sharp, out_0, out_1):
                 out=attn3[:, P * a:P * (a + 1), P * b:P * (b + 1)].rearrange("n p c -> p n c"),
                 in_=rng[b][:, a, :, :])
 
-        def block(i, j):
-            banks = []
-            for hh in range(2):
-                bank = psum.tile([P, 4, P], F32, name="sc", tag="sc")
-                for nn in range(4):
-                    n = 4 * hh + nn
-                    for u in range(4):
-                        for e in range(2):
-                            nc.tensor.matmul(out=bank[:, nn, :], lhsT=qtb(i, n, u, e), rhs=qtb(j, n, u, e),
-                                             start=(u == 0 and e == 0), stop=(u == 3 and e == 1))
-                banks.append(bank)
+        sc = {}
+        dts = {}
+
+        def pe_scores(s):
+            i, j = BLOCKS[s]
+            pair = [bank(2 * (s % 3)), bank(2 * (s % 3) + 1)]
+            sc[s] = pair
+            for n in range(H):
+                for u in range(4):
+                    for e in range(2):
+                        nc.tensor.matmul(out=pair[n // 4][:, n % 4, :], lhsT=qtb(i, n, u, e), rhs=qtb(j, n, u, e),
+                                         start=(u == 0 and e == 0), stop=(u == 3 and e == 1))
+                if s < 3:
+                    x_transpose_bank(s + 1, n, 6 + n % 2, "v" if (s == 0 and n % 2 == 1) else "s")
+
+        def maxsub(s):
+            pair = sc[s]
             pm = small.tile([P, 2, P], F32, name="pm", tag="pm")
             for hh in range(2):
-                nc.vector.tensor_reduce(out=pm[:, hh, :], in_=banks[hh][:].rearrange("p h c -> p c h"),
+                nc.vector.tensor_reduce(out=pm[:, hh, :], in_=pair[hh][:].rearrange("p h c -> p c h"),
                                         axis=AX.X, op=ALU.max)
             m = small.tile([P, P], F32, name="m", tag="m")
-            nc.vector.tensor_tensor(out=m[:], in0=pm[:, 0, :], in1=pm[:, 1, :], op=ALU.max)
+            if MULT_G or RG_G:
+                nc.vector.tensor_reduce(out=m[:], in_=pm[:].rearrange("p h c -> p c h"), axis=AX.X, op=ALU.max)
+            else:
+                nc.vector.tensor_tensor(out=m[:], in0=pm[:, 0, :], in1=pm[:, 1, :], op=ALU.max)
             d = dpool.tile([P, H, P], F32, name="d", tag="d")
+            dts[s] = d
             for hh in range(2):
-                nc.vector.tensor_tensor(out=d[:, 4 * hh:4 * (hh + 1), :], in0=banks[hh][:],
+                nc.vector.tensor_tensor(out=d[:, 4 * hh:4 * (hh + 1), :], in0=pair[hh][:],
                                         in1=m[:].unsqueeze(1).to_broadcast([P, 4, P]), op=ALU.subtract)
+
+        def expo(s):
+            d = dts[s]
             nc.scalar.activation(out=d[:], in_=d[:], func=ACT.Exp, scale=rg[:, 0:1])
+
+        def fin(s):
+            i, j = BLOCKS[s]
+            d = dts[s]
             z = small.tile([P, P], F32, name="z", tag="z")
             nc.vector.tensor_reduce(out=z[:], in_=d[:].rearrange("p h c -> p c h"), axis=AX.X, op=ALU.add)
             r = small.tile([P, P], F32, name="r", tag="r")
             nc.vector.reciprocal(out=r[:], in_=z[:])
-            nc.gpsimd.tensor_tensor(out=rng[j][:, i, :, :], in0=d[:],
-                                    in1=r[:].unsqueeze(1).to_broadcast([P, H, P]), op=ALU.mult)
+            eng = nc.gpsimd if MULT_G else nc.vector
+            eng.tensor_tensor(out=rng[j][:, i, :, :], in0=d[:],
+                              in1=r[:].unsqueeze(1).to_broadcast([P, H, P]), op=ALU.mult)
             store_block(i, j)
-            if i < j:
-                for hh in range(2):
-                    tb = psum.tile([P, 4, P], F32, name="tb", tag="tp")
-                    for nn in range(4):
-                        nc.tensor.transpose(tb[:, nn, :], rng[j][:, i, 4 * hh + nn, :], ident[:])
-                    nc.scalar.copy(out=rng[i][:, j, 4 * hh:4 * (hh + 1), :], in_=tb[:])
-                store_block(j, i)
 
-        def quantise_range(j, ac, asc, engines):
-            for k in range(4):
-                ga = stage.tile([P, 2, P, 4], BF16, name="ga", tag="ga", bufs=4, align_bytes=64)
-                src = rng[j][:, :, 2 * k:2 * (k + 1), :].rearrange("p t n c -> p n c t")
-                if engines[k] == "v":
-                    nc.vector.tensor_copy(out=ga[:], in_=src)
-                else:
-                    nc.scalar.copy(out=ga[:], in_=src)
-                for nn in range(2):
-                    n = 2 * k + nn
-                    nc.vector.quantize_mx(out=ac[:, n, P * j:P * (j + 1)].bitcast(FP8X4),
-                                          scales=asc[:, n, P * j:P * (j + 1)],
-                                          in_=ga[:, nn, :, :].rearrange("p c t -> p (c t)"))
-
-        for t in range(T):
-            x_transposes(t)
-            block(0, t)
-        for j in range(1, T):
-            block(1, j)
-        ac = big.tile([P, H, C], U32, name="ac", offset=80 * KIB, align_bytes=64)
-        asc = big.tile([P, H, C], U8, name="asc", offset=74 * KIB, align_bytes=64)
-        quantise_range(0, ac, asc, "ssss")
-        quantise_range(1, ac, asc, "ssss")
-        block(2, 2)
-        block(2, 3)
-        quantise_range(2, ac, asc, "ssss")
-        block(3, 3)
-        quantise_range(3, ac, asc, "vsvs")
-
-        qc_off = [64, 0, 16, 32]
-        qc = []
-        qs = []
-        for hp in range(4):
-            qc_t = big.tile([P, 2, WD], U32, name="qc%d" % hp, offset=qc_off[hp] * KIB, align_bytes=64)
-            qs_t = big.tile([P, 2, WD], U8, name="qs%d" % hp, offset=(qc_off[hp] + 8) * KIB, align_bytes=64)
-            qc.append(qc_t)
-            qs.append(qs_t)
+        def xpose(s):
+            i, j = BLOCKS[s]
+            if i == j:
+                return
             for hh in range(2):
-                xv = xs[hp][:, :, WD * hh:WD * (hh + 1)].rearrange("p t (m r) -> p r m t", r=8)
-                for a in range(2):
-                    gq = stage.tile([P, 4, P, 4], BF16, name="gq", tag="gq", bufs=2, align_bytes=64)
-                    nc.gpsimd.tensor_scalar(out=gq[:], in0=xv[:, 4 * a:4 * (a + 1), :, :], scalar1=1.0, scalar2=0.0,
-                                            op0=ALU.mult, op1=ALU.add)
-                    nc.vector.quantize_mx(out=qc_t[:, hh, 512 * a:512 * (a + 1)].bitcast(FP8X4),
-                                          scales=qs_t[:, hh, 512 * a:512 * (a + 1)],
-                                          in_=gq[:].rearrange("p r m t -> p (r m t)"))
+                tb = bank(6 + hh)
+                for nn in range(4):
+                    nc.tensor.transpose(tb[:, nn, :], rng[j][:, i, 4 * hh + nn, :], ident[:])
+                nc.scalar.copy(out=rng[i][:, j, 4 * hh:4 * (hh + 1), :], in_=tb[:])
+            store_block(j, i)
 
-        h_off = [96, 104, 112, 120, 128, 136, 144, 152, 160, 168, 176, 184, 96, 104, 112, 120]
+        gas = {}
+        acs = []
+
+        def t4(j, k, eng):
+            ga = stage.tile([P, 2, P, 4], BF16, name="ga", tag="ga", align_bytes=64)
+            gas[(j, k)] = ga
+            copy_on(eng, ga[:], rng[j][:, :, 2 * k:2 * (k + 1), :].rearrange("p t n c -> p n c t"))
+
+        def t5(j, k):
+            ga = gas[(j, k)]
+            ac = acs[0]
+            for nn in range(2):
+                n = 2 * k + nn
+                nc.vector.quantize_mx(out=ac[:, n, P * j:P * (j + 1)].bitcast(FP8X4),
+                                      scales=asc[:, n, P * j:P * (j + 1)],
+                                      in_=ga[:, nn, :, :].rearrange("p c t -> p (c t)"))
+
+        gq_off = [64, 0, 16, 32]
+        gqp = {}
+
+        def regroup(q, eng):
+            n = q // 2
+            a = q % 2
+            hp = n // 2
+            if hp not in gqp:
+                gqp[hp] = big.tile([P, 2, 8, P, 4], BF16, name="gq%d" % hp, offset=gq_off[hp] * KIB, align_bytes=64)
+            xv = xs[hp][:, :, WD * (n % 2):WD * (n % 2 + 1)].rearrange("p t (m r) -> p r m t", r=8)
+            dst = gqp[hp][:, n % 2, 4 * a:4 * (a + 1), :, :]
+            src = xv[:, 4 * a:4 * (a + 1), :, :]
+            if eng == "g":
+                nc.gpsimd.tensor_scalar(out=dst, in0=src, scalar1=1.0, scalar2=0.0, op0=ALU.mult, op1=ALU.add)
+            else:
+                copy_on(eng, dst, src)
+
+        qcodes = {}
+
+        def quantise_q(n):
+            if n < 2:
+                codes = qc01[:, n, :]
+                scales = qs01[:, n, :]
+            else:
+                base = (64 + 5 * (n - 2)) if n < 5 else 5 * (n - 5)
+                qc_t = big.tile([P, WD], U32, name="qc%d" % n, offset=base * KIB, align_bytes=64)
+                qs_t = big.tile([P, WD], U8, name="qs%d" % n, offset=(base + 4) * KIB, align_bytes=64)
+                codes = qc_t[:]
+                scales = qs_t[:]
+            qcodes[n] = (codes, scales)
+            nc.vector.quantize_mx(out=codes.bitcast(FP8X4), scales=scales,
+                                  in_=gqp[n // 2][:, n % 2, :, :, :].rearrange("p r m t -> p (r m t)"))
+
         for n in range(H):
+            x_transpose_bank(0, n, n, "v" if n % 2 == 1 else "s")
+
+        for s in range(len(BLOCKS) + XLAG):
+            if s < len(BLOCKS):
+                pe_scores(s)
+                maxsub(s)
+                expo(s)
+            if 1 <= s <= len(BLOCKS):
+                fin(s - 1)
+            if XLAG <= s:
+                xpose(s - XLAG)
+            if s == 6:
+                acs.append(big.tile([P, H, C], U32, name="ac", offset=80 * KIB, align_bytes=64))
+                t4(0, 0, "s")
+                t4(0, 1, "s")
+            if s == 7:
+                t4(0, 2, "s")
+                t4(0, 3, "s")
+            if s == 8:
+                for k in range(4):
+                    t5(0, k)
+            if s == 9:
+                for k in range(4):
+                    t4(1, k, "s")
+            if s == 10:
+                for k in range(4):
+                    t5(1, k)
+            if RG_G:
+                if 3 <= s <= 10:
+                    regroup(s - 3, "g")
+                if s == 11:
+                    for q in range(8, 16):
+                        regroup(q, "g")
+            else:
+                if 3 <= s <= 6:
+                    regroup(s - 3, "s")
+            if s == 6:
+                quantise_q(0)
+            if s == 8:
+                quantise_q(1)
+
+        h_off = [96, 104, 112, 120, 128, 136, 144, 152, 96, 104, 112, 120, 160, 168, 176, 184]
+        for n in range(H):
+            if n % 2 == 0:
+                k = n // 2
+                t4(2, k, "s")
+                t4(3, k, "v")
+                t5(2, k)
+                t5(3, k)
+            codes, scales = qcodes[n]
+            ac = acs[0]
             hv = h2[WD * n:WD * (n + 1), :].rearrange("(m r) c -> m r c", r=8)
             for a in range(2):
+                if n + 2 < H and not RG_G:
+                    regroup(2 * (n + 2) + a, "v")
                 hsb = big.tile([P, 4, C], F32, name="h%d_%d" % (n, a), offset=h_off[2 * n + a] * KIB, align_bytes=64)
                 for rr in range(4):
                     r8 = 4 * a + rr
-                    bank = psum.tile([P, C], F32, name="hb", tag=("tp" if rr % 2 == 0 else "sc"))
-                    nc.tensor.matmul_mx(out=bank[:],
-                                        lhsT=qc[n // 2][:, n % 2, P * r8:P * (r8 + 1)].bitcast(FP8X4),
-                                        lhsT_scale=qs[n // 2][:, n % 2, P * r8:P * (r8 + 1)],
+                    bk = bank(r8)
+                    flat = bk[:].rearrange("p a b -> p (a b)")
+                    nc.tensor.matmul_mx(out=flat,
+                                        lhsT=codes[:, P * r8:P * (r8 + 1)].bitcast(FP8X4),
+                                        lhsT_scale=scales[:, P * r8:P * (r8 + 1)],
                                         rhs=ac[:, n, :].bitcast(FP8X4),
                                         rhs_scale=asc[:, n, :],
                                         start=True, stop=True)
-                    if rr % 2 == 0:
-                        nc.scalar.copy(out=hsb[:, rr, :], in_=bank[:])
+                    if RG_G or n + 2 >= H:
+                        eng = "v" if rr % 2 == 1 else "s"
                     else:
-                        nc.vector.tensor_copy(out=hsb[:, rr, :], in_=bank[:])
+                        eng = "v" if rr == 3 else "s"
+                    copy_on(eng, hsb[:, rr, :], flat)
                 nc.sync.dma_start(out=hv[:, 4 * a:4 * (a + 1), :], in_=hsb[:])
+            if n + 2 < H:
+                quantise_q(n + 2)

@@ -132,8 +132,11 @@ def tile_channelgroupattention_pa_kernel(tc, qkv_bn, gra_sharp, out_0, out_1):
         def fin(s):
             i, j = BLOCKS[s]
             d = dts[s]
+            t1 = small.tile([P, 4, P], F32, name="t1", tag="t1", bufs=1)
+            nc.vector.tensor_tensor(out=t1[:], in0=d[:, 0:4, :], in1=d[:, 4:8, :], op=ALU.add)
+            nc.vector.tensor_tensor(out=t1[:, 0:2, :], in0=t1[:, 0:2, :], in1=t1[:, 2:4, :], op=ALU.add)
             z = small.tile([P, P], F32, name="z", tag="z")
-            nc.vector.tensor_reduce(out=z[:], in_=d[:].rearrange("p h c -> p c h"), axis=AX.X, op=ALU.add)
+            nc.vector.tensor_tensor(out=z[:], in0=t1[:, 0, :], in1=t1[:, 1, :], op=ALU.add)
             r = small.tile([P, P], F32, name="r", tag="r")
             nc.vector.reciprocal(out=r[:], in_=z[:])
             eng = nc.gpsimd if MULT_G else nc.vector
@@ -178,9 +181,9 @@ def tile_channelgroupattention_pa_kernel(tc, qkv_bn, gra_sharp, out_0, out_1):
             hp = n // 2
             if hp not in gqp:
                 gqp[hp] = big.tile([P, 2, 8, P, 4], BF16, name="gq%d" % hp, offset=gq_off[hp] * KIB, align_bytes=64)
-            xv = xs[hp][:, :, WD * (n % 2):WD * (n % 2 + 1)].rearrange("p t (m r) -> p r m t", r=8)
-            dst = gqp[hp][:, n % 2, 4 * a:4 * (a + 1), :, :]
-            src = xv[:, 4 * a:4 * (a + 1), :, :]
+            base = WD * (n % 2) + 512 * a
+            src = xs[hp][:, :, base:base + 512].rearrange("p t (m i) -> p m t i", i=4)
+            dst = gqp[hp][:, n % 2, 4 * a:4 * (a + 1), :, :].rearrange("p i m t -> p m t i")
             if eng == "g":
                 nc.gpsimd.tensor_scalar(out=dst, in0=src, scalar1=1.0, scalar2=0.0, op0=ALU.mult, op1=ALU.add)
             else:
@@ -254,7 +257,6 @@ def tile_channelgroupattention_pa_kernel(tc, qkv_bn, gra_sharp, out_0, out_1):
                 t5(3, k)
             codes, scales = qcodes[n]
             ac = acs[0]
-            hv = h2[WD * n:WD * (n + 1), :].rearrange("(m r) c -> m r c", r=8)
             for a in range(2):
                 if n + 2 < H and not RG_G:
                     regroup(2 * (n + 2) + a, "v")
@@ -272,8 +274,9 @@ def tile_channelgroupattention_pa_kernel(tc, qkv_bn, gra_sharp, out_0, out_1):
                     if RG_G or n + 2 >= H:
                         eng = "v" if rr % 2 == 1 else "s"
                     else:
-                        eng = "v" if rr == 3 else "s"
+                        eng = "v" if (rr == 3 and a == 1) else "s"
                     copy_on(eng, hsb[:, rr, :], flat)
-                nc.sync.dma_start(out=hv[:, 4 * a:4 * (a + 1), :], in_=hsb[:])
+                hv = h2[WD * n + 512 * a:WD * n + 512 * (a + 1), :].rearrange("(m r) c -> m r c", r=4)
+                nc.sync.dma_start(out=hv, in_=hsb[:])
             if n + 2 < H:
                 quantise_q(n + 2)

@@ -21,9 +21,9 @@ KIB = 1024
 
 FLOPS = 2 * 2 * H * C * C * WD
 
-MULT_G = False
-RG_G = False
-BLOCKS = [(0, 0), (0, 1), (0, 2), (0, 3), (1, 1), (1, 2), (1, 3), (2, 2), (2, 3), (3, 3)]
+MULT_G = True
+BLOCKS = [(0, 0), (0, 1), (0, 2), (0, 3), (1, 2), (1, 3), (1, 1), (2, 3), (2, 2), (3, 3)]
+NB = len(BLOCKS)
 XLAG = 3
 
 
@@ -96,6 +96,10 @@ def tile_channelgroupattention_pa_kernel(tc, qkv_bn, gra_sharp, out_0, out_1):
         sc = {}
         dts = {}
 
+        def expo(s):
+            d = dts[s]
+            nc.scalar.activation(out=d[:], in_=d[:], func=ACT.Exp, scale=rg[:, 0:1])
+
         def pe_scores(s):
             i, j = BLOCKS[s]
             pair = [bank(2 * (s % 3)), bank(2 * (s % 3) + 1)]
@@ -107,6 +111,8 @@ def tile_channelgroupattention_pa_kernel(tc, qkv_bn, gra_sharp, out_0, out_1):
                                          start=(u == 0 and e == 0), stop=(u == 3 and e == 1))
                 if s < 3:
                     x_transpose_bank(s + 1, n, 6 + n % 2, "v" if (s == 0 and n % 2 == 1) else "s")
+                if 1 <= s <= 3 and n == 3:
+                    expo(s - 1)
 
         def maxsub(s):
             pair = sc[s]
@@ -115,7 +121,7 @@ def tile_channelgroupattention_pa_kernel(tc, qkv_bn, gra_sharp, out_0, out_1):
                 nc.vector.tensor_reduce(out=pm[:, hh, :], in_=pair[hh][:].rearrange("p h c -> p c h"),
                                         axis=AX.X, op=ALU.max)
             m = small.tile([P, P], F32, name="m", tag="m")
-            if MULT_G or RG_G:
+            if MULT_G:
                 nc.vector.tensor_reduce(out=m[:], in_=pm[:].rearrange("p h c -> p c h"), axis=AX.X, op=ALU.max)
             else:
                 nc.vector.tensor_tensor(out=m[:], in0=pm[:, 0, :], in1=pm[:, 1, :], op=ALU.max)
@@ -124,10 +130,6 @@ def tile_channelgroupattention_pa_kernel(tc, qkv_bn, gra_sharp, out_0, out_1):
             for hh in range(2):
                 nc.vector.tensor_tensor(out=d[:, 4 * hh:4 * (hh + 1), :], in0=pair[hh][:],
                                         in1=m[:].unsqueeze(1).to_broadcast([P, 4, P]), op=ALU.subtract)
-
-        def expo(s):
-            d = dts[s]
-            nc.scalar.activation(out=d[:], in_=d[:], func=ACT.Exp, scale=rg[:, 0:1])
 
         def fin(s):
             i, j = BLOCKS[s]
@@ -144,7 +146,7 @@ def tile_channelgroupattention_pa_kernel(tc, qkv_bn, gra_sharp, out_0, out_1):
                               in1=r[:].unsqueeze(1).to_broadcast([P, H, P]), op=ALU.mult)
             store_block(i, j)
 
-        def xpose(s):
+        def mirror(s):
             i, j = BLOCKS[s]
             if i == j:
                 return
@@ -164,6 +166,8 @@ def tile_channelgroupattention_pa_kernel(tc, qkv_bn, gra_sharp, out_0, out_1):
             copy_on(eng, ga[:], rng[j][:, :, 2 * k:2 * (k + 1), :].rearrange("p t n c -> p n c t"))
 
         def t5(j, k):
+            if not acs:
+                acs.append(big.tile([P, H, C], U32, name="ac", offset=80 * KIB, align_bytes=64))
             ga = gas[(j, k)]
             ac = acs[0]
             for nn in range(2):
@@ -184,10 +188,7 @@ def tile_channelgroupattention_pa_kernel(tc, qkv_bn, gra_sharp, out_0, out_1):
             base = WD * (n % 2) + 512 * a
             src = xs[hp][:, :, base:base + 512].rearrange("p t (m i) -> p m t i", i=4)
             dst = gqp[hp][:, n % 2, 4 * a:4 * (a + 1), :, :].rearrange("p i m t -> p m t i")
-            if eng == "g":
-                nc.gpsimd.tensor_scalar(out=dst, in0=src, scalar1=1.0, scalar2=0.0, op0=ALU.mult, op1=ALU.add)
-            else:
-                copy_on(eng, dst, src)
+            copy_on(eng, dst, src)
 
         qcodes = {}
 
@@ -208,57 +209,47 @@ def tile_channelgroupattention_pa_kernel(tc, qkv_bn, gra_sharp, out_0, out_1):
         for n in range(H):
             x_transpose_bank(0, n, n, "v" if n % 2 == 1 else "s")
 
-        for s in range(len(BLOCKS) + XLAG):
-            if s < len(BLOCKS):
+        for s in range(NB + XLAG):
+            for j in range(2):
+                u = s - (7 + 2 * j)
+                if u == 0 or u == 1:
+                    t4(j, 2 * u, "s")
+                    t4(j, 2 * u + 1, "s")
+            if 4 <= s <= 9:
+                regroup(s - 4, "s")
+            if s < NB:
                 pe_scores(s)
                 maxsub(s)
-                expo(s)
-            if 1 <= s <= len(BLOCKS):
-                fin(s - 1)
-            if XLAG <= s:
-                xpose(s - XLAG)
-            if s == 6:
-                acs.append(big.tile([P, H, C], U32, name="ac", offset=80 * KIB, align_bytes=64))
-                t4(0, 0, "s")
-                t4(0, 1, "s")
-            if s == 7:
-                t4(0, 2, "s")
-                t4(0, 3, "s")
+                if s >= 3:
+                    expo(s)
+            if s == 6 or s == 8:
+                quantise_q((s - 6) // 2)
             if s == 8:
                 for k in range(4):
                     t5(0, k)
-            if s == 9:
-                for k in range(4):
-                    t4(1, k, "s")
+            if 1 <= s <= NB:
+                fin(s - 1)
+            if XLAG <= s:
+                mirror(s - XLAG)
             if s == 10:
                 for k in range(4):
                     t5(1, k)
-            if RG_G:
-                if 3 <= s <= 10:
-                    regroup(s - 3, "g")
-                if s == 11:
-                    for q in range(8, 16):
-                        regroup(q, "g")
-            else:
-                if 3 <= s <= 6:
-                    regroup(s - 3, "s")
-            if s == 6:
-                quantise_q(0)
-            if s == 8:
-                quantise_q(1)
+
+        def last_ranges(k):
+            t4(2, k, "s")
+            t4(3, k, "v")
+            t5(2, k)
+            t5(3, k)
 
         h_off = [96, 104, 112, 120, 128, 136, 144, 152, 96, 104, 112, 120, 160, 168, 176, 184]
+        last_ranges(0)
         for n in range(H):
-            if n % 2 == 0:
-                k = n // 2
-                t4(2, k, "s")
-                t4(3, k, "v")
-                t5(2, k)
-                t5(3, k)
             codes, scales = qcodes[n]
             ac = acs[0]
             for a in range(2):
-                if n + 2 < H and not RG_G:
+                if n % 2 == 0 and a == 1 and n // 2 + 1 < 4:
+                    last_ranges(n // 2 + 1)
+                if 3 <= n + 2 < H:
                     regroup(2 * (n + 2) + a, "v")
                 hsb = big.tile([P, 4, C], F32, name="h%d_%d" % (n, a), offset=h_off[2 * n + a] * KIB, align_bytes=64)
                 for rr in range(4):
@@ -271,7 +262,7 @@ def tile_channelgroupattention_pa_kernel(tc, qkv_bn, gra_sharp, out_0, out_1):
                                         rhs=ac[:, n, :].bitcast(FP8X4),
                                         rhs_scale=asc[:, n, :],
                                         start=True, stop=True)
-                    if RG_G or n + 2 >= H:
+                    if n + 2 >= H:
                         eng = "v" if rr % 2 == 1 else "s"
                     else:
                         eng = "v" if (rr == 3 and a == 1) else "s"

@@ -141,7 +141,7 @@ def tile_channelgroupattention_pa_kernel(tc, qkv_bn, gra_sharp, out_0, out_1):
             nc.vector.tensor_tensor(out=z[:], in0=t1[:, 0, :], in1=t1[:, 1, :], op=ALU.add)
             r = small.tile([P, P], F32, name="r", tag="r")
             nc.vector.reciprocal(out=r[:], in_=z[:])
-            eng = nc.gpsimd if MULT_G else nc.vector
+            eng = nc.gpsimd if (MULT_G and s < NB - 1) else nc.vector
             eng.tensor_tensor(out=rng[j][:, i, :, :], in0=d[:],
                               in1=r[:].unsqueeze(1).to_broadcast([P, H, P]), op=ALU.mult)
             store_block(i, j)
@@ -163,7 +163,8 @@ def tile_channelgroupattention_pa_kernel(tc, qkv_bn, gra_sharp, out_0, out_1):
         def t4(j, k, eng):
             ga = stage.tile([P, 2, P, 4], BF16, name="ga", tag="ga", align_bytes=64)
             gas[(j, k)] = ga
-            copy_on(eng, ga[:], rng[j][:, :, 2 * k:2 * (k + 1), :].rearrange("p t n c -> p n c t"))
+            copy_on(eng, ga[:].rearrange("p n (q i) t -> p (n q) t i", i=4),
+                    rng[j][:, :, 2 * k:2 * (k + 1), :].rearrange("p t n (q i) -> p (n q) t i", i=4))
 
         def t5(j, k):
             if not acs:

@@ -21,10 +21,69 @@ KIB = 1024
 
 FLOPS = 2 * 2 * H * C * C * WD
 
-MULT_G = True
-BLOCKS = [(0, 0), (0, 1), (0, 2), (0, 3), (1, 2), (1, 3), (1, 1), (2, 3), (2, 2), (3, 3)]
+
+BLOCKS = [(0, 0), (1, 0), (2, 0), (3, 0), (1, 1), (2, 1), (3, 1), (2, 2), (3, 2), (3, 3)]
 NB = len(BLOCKS)
-XLAG = 3
+LOADS = [(t, hp) for t in (0, 1) for hp in range(4)] + [(2, 0), (3, 0), (2, 1), (2, 2), (2, 3), (3, 1), (3, 2), (3, 3)]
+GROUPS = [(0, 256), (2, 256)]
+LATE = [6, 7, 2, 3, 6, 7, 2, 3]
+ROTATE = [4, 5, 0, 1, 6, 7, 2, 3]
+CODE_OFF = [0, 5, 10, 16, 21, 26, 32, 37]
+H_OFF = [80, 84, 88, 92, 96, 100, 104, 108, 112, 116, 120, 124]
+R4 = range(4)
+R8 = range(8)
+
+
+def soft(s):
+    return ["A%d0" % s, "A%d1" % s, "X%d" % s, "B%d0" % s, "B%d1" % s]
+
+
+def gsum(s):
+    return ["G%d0" % s, "G%d1" % s, "G%d2" % s]
+
+
+def tree(s):
+    return ["D%d0" % s, "D%d1" % s, "D%d2" % s]
+
+
+def ca(n, bs=R4):
+    return ["cH%d0%d" % (n, b) for b in bs]
+
+
+def cb(n, bs=(0, 2)):
+    return ["cH%d1%d" % (n, b) for b in bs]
+
+
+def scores(s):
+    return ["S%d%d" % (s, n) for n in R8]
+
+
+def programs():
+    t = ['T0%d' % n for n in R8]
+    for b, u in ((0, 1), (1, 2), (2, 3)):
+        for n in R8:
+            t += ['S%d%d' % (b, n), 'T%d%d' % (u, n)]
+    for b in (3, 4, 5):
+        t += scores(b)
+    t += ['M10', 'M11'] + scores(6) + ['M20', 'M21'] + scores(7) + ['M30', 'M31'] + scores(8) + scores(9)
+    ha = [['H%d0%d' % (n, b) for b in R4] for n in R8]
+    hb = [['H%d1%d' % (n, b) for b in R4] for n in R8]
+    t += ha[0] + ha[1] + ha[2] + ['M50', 'M51', 'M60', 'M61'] + ha[3] + ['M80', 'M81'] + ha[4] + hb[0] + hb[1] + hb[2] + hb[3] + ha[5] + ha[6] + hb[4] + hb[5] + ha[7] + hb[6] + hb[7]
+    v = ['cT01', 'cT03', 'cT05', 'cT07', 'cT11', 'cT13', 'cT15', 'A00', 'cT17', 'A01', 'X0', 'B00', 'B01', 'A10', 'A11', 'X1', 'B10', 'B11', 'Q0', 'cT33', 'A20', 'cT35', 'A21', 'R0', 'X2', 'cT37', 'B20', 'B21', 'Q1']
+    for b in (3, 4, 5, 6):
+        v += ['A%d0' % b, 'A%d1' % b, 'R%d' % (b - 2), 'X%d' % b, 'B%d0' % b, 'B%d1' % b]
+        if b == 4:
+            v += ['Q2']
+    v += ['A70', 'A71', 'F60', 'F61', 'Z00', 'R5', 'F62', 'X7', 'A80', 'R6', 'A81', 'U6', 'X8', 'B70', 'Z01', 'B71', 'Z02', 'A90', 'Z03', 'Z10', 'B80', 'A91', 'B81', 'X9', 'R7', 'Z11', 'B90', 'B91']
+    v += tree(8) + ['R8', 'Q3', 'cH203', 'K8', 'D90', 'U8', 'D91', 'Z12', 'D92', 'K9', 'R9', 'Q4', 'U9', 'cH303', 'Z13', 'cH403', 'Z20', 'Z30']
+    v += ['cH011', 'cH013', 'K10', 'cH111', 'cH113', 'Z21', 'Z31', 'K11', 'Q5', 'cH211', 'cH213', 'K12', 'cH311', 'cH313', 'K13', 'Q6', 'cH503', 'Z22', 'Z32', 'K14', 'cH603', 'K15', 'Q7', 'cH411', 'cH413', 'cH511', 'cH513', 'cH703', 'Z23', 'Z33', 'cH611', 'cH613', 'cH711', 'cH713']
+    s = ['cT00', 'cT02', 'cT04', 'cT06', 'cT10', 'cT12', 'cT14', 'cT16', 'cT20', 'cT21', 'cT22', 'cT23', 'E0', 'cT24', 'cT25', 'cT26', 'cT27', 'cT30', 'cT31', 'E1', 'cT32', 'cT34', 'cT36', 'K4', 'E2']
+    s += ['K5', 'E3', 'K6', 'E4', 'cM10', 'cM11', 'K7', 'E5', 'cM20', 'cM21', 'P00', 'E6', 'P01', 'P02', 'P03', 'cM30', 'cM31', 'P10', 'E7', 'P11']
+    s += ca(0) + ['E8'] + ca(1) + ['E9', 'P12'] + ca(2, range(3)) + ['cM50', 'cM51', 'P13', 'cM60', 'cM61'] + ca(3, range(3)) + ['cM80', 'cM81', 'P30'] + ca(4, range(3)) + ['P31'] + cb(0) + cb(1) + cb(2) + cb(3) + ['P32'] + ca(5, range(3)) + ca(6, range(3)) + ['P33'] + cb(4) + cb(5) + ca(7, range(3)) + cb(6) + cb(7)
+    g = ['K0', 'K1', 'K2', 'K3'] + gsum(0) + gsum(1) + ['U0'] + gsum(2) + ['U1'] + gsum(3) + ['U2'] + gsum(4) + ['U3'] + gsum(5) + ['U4', 'U5'] + gsum(7) + ['U7', 'P20', 'P21', 'P22', 'P23']
+    q = ["a0", "a1", "b1", "a2", "b2", "a3", "a4", "b3", "a5", "a6", "h000", "h001", "h100", "h101", "a7", "h200", "h201", "b5", "a8", "b6", "h300", "h301", "b8", "a9"]
+    q += ["h%d%d%d" % (n, grp, x) for n, grp in ((4, 0), (0, 1), (1, 1), (2, 1), (3, 1), (5, 0), (6, 0), (4, 1), (5, 1), (7, 0), (6, 1), (7, 1)) for x in range(2)]
+    return {"t": t, "v": v, "s": s, "g": g, "q": q}
 
 
 def tile_channelgroupattention_pa_kernel(tc, qkv_bn, gra_sharp, out_0, out_1):
@@ -36,18 +95,14 @@ def tile_channelgroupattention_pa_kernel(tc, qkv_bn, gra_sharp, out_0, out_1):
     with ExitStack() as ctx:
         big = ctx.enter_context(tc.tile_pool(name="big", bufs=1))
         const = ctx.enter_context(tc.tile_pool(name="const", bufs=1))
-        small = ctx.enter_context(tc.tile_pool(name="small", bufs=2))
-        dpool = ctx.enter_context(tc.tile_pool(name="dpool", bufs=3))
-        stage = ctx.enter_context(tc.tile_pool(name="stage", bufs=4))
+        small = ctx.enter_context(tc.tile_pool(name="small", bufs=1))
+        stage = ctx.enter_context(tc.tile_pool(name="stage", bufs=1))
         psum = ctx.enter_context(tc.psum_pool(name="psum", bufs=1))
         ctx.enter_context(tc.manual_schedule())
 
-        xs = [big.tile([P, T, 2 * WD], BF16, name="x%d" % hp, offset=hp * 16 * KIB, align_bytes=64)
-              for hp in range(4)]
-        qt = [big.tile([P, H, 4, P], F32, name="qt%d" % t, offset=(64 + 16 * t) * KIB, align_bytes=64)
-              for t in range(T)]
-        rng = [big.tile([P, T, H, P], F32, name="rng%d" % j, offset=(128 + 16 * j) * KIB, align_bytes=64)
-               for j in range(T)]
+        xs = [big.tile([P, T, 2 * WD], BF16, name="x%d" % hp, offset=hp * 16 * KIB, align_bytes=64) for hp in range(4)]
+        qt = [big.tile([P, H, 4, P], F32, name="qt%d" % t, offset=(64 + 16 * t) * KIB, align_bytes=64) for t in range(T)]
+        rng = [big.tile([P, T, H, P], F32, name="rng%d" % j, offset=(128 + 16 * j) * KIB, align_bytes=64) for j in range(T)]
 
         ident = const.tile([P, P], F32, name="ident")
         make_identity(nc, ident[:])
@@ -59,13 +114,17 @@ def tile_channelgroupattention_pa_kernel(tc, qkv_bn, gra_sharp, out_0, out_1):
         rg = const.tile([P, 1], F32, name="rg")
         nc.vector.reciprocal(out=rg[:], in_=g_f[:])
         asc = const.tile([P, H, C], U8, name="asc", align_bytes=64)
-        qc01 = const.tile([P, 2, WD], U32, name="qc01", align_bytes=64)
-        qs01 = const.tile([P, 2, WD], U8, name="qs01", align_bytes=64)
 
-        for t in range(T):
-            for hp in range(4):
-                nc.sync.dma_start(out=xs[hp][:, t, :],
-                                  in_=x[P * t:P * (t + 1), 2 * WD * hp:2 * WD * (hp + 1)])
+        for t, hp in LOADS:
+            nc.sync.dma_start(out=xs[hp][:, t, :], in_=x[P * t:P * (t + 1), 2 * WD * hp:2 * WD * (hp + 1)])
+
+        prog = programs()
+        where = {}
+        for e in prog:
+            for name in prog[e]:
+                where[name] = e
+        tiles = {}
+        ops = {}
 
         def bank(idx):
             return psum.tile([P, 4, P], F32, name="bk%d" % idx, tag="bk%d" % idx)
@@ -76,199 +135,291 @@ def tile_channelgroupattention_pa_kernel(tc, qkv_bn, gra_sharp, out_0, out_1):
             else:
                 nc.scalar.copy(out=out, in_=in_)
 
-        def x_transpose_bank(t, n, idx, eng):
-            tb = bank(idx)
-            base = WD * (n % 2)
-            for u in range(4):
-                nc.tensor.transpose(tb[:, u, :],
-                                    xs[n // 2][:, t, base + 256 * u:base + 256 * (u + 1)].bitcast(F32),
-                                    ident[:])
-            copy_on(eng, qt[t][:, n, :, :], tb[:])
-
         def qtb(t, n, u, e):
             return qt[t][:, n, u, :].bitcast(BF16).rearrange("p (c e) -> p c e", e=2)[:, :, e]
 
-        def store_block(a, b):
-            nc.sync.dma_start(
-                out=attn3[:, P * a:P * (a + 1), P * b:P * (b + 1)].rearrange("n p c -> p n c"),
-                in_=rng[b][:, a, :, :])
+        def transpose_x(name, t, n, idx):
+            def emit(eng):
+                tb = bank(idx)
+                tiles[name] = tb
+                base = WD * (n % 2)
+                for u in range(4):
+                    nc.tensor.transpose(tb[:, u, :], xs[n // 2][:, t, base + 256 * u:base + 256 * (u + 1)].bitcast(F32), ident[:])
+            return emit
 
-        sc = {}
-        dts = {}
+        def copy_x(name, t, n):
+            def emit(eng):
+                copy_on(eng, qt[t][:, n, :, :], tiles[name][:])
+            return emit
 
-        def expo(s):
-            d = dts[s]
-            nc.scalar.activation(out=d[:], in_=d[:], func=ACT.Exp, scale=rg[:, 0:1])
-
-        def pe_scores(s):
-            i, j = BLOCKS[s]
-            pair = [bank(2 * (s % 3)), bank(2 * (s % 3) + 1)]
-            sc[s] = pair
-            for n in range(H):
+        def score(s, n, idx):
+            def emit(eng):
+                i, j = BLOCKS[s]
+                if n % 4 == 0:
+                    tiles["sc%d%d" % (s, n // 4)] = bank(idx)
                 for u in range(4):
                     for e in range(2):
-                        nc.tensor.matmul(out=pair[n // 4][:, n % 4, :], lhsT=qtb(i, n, u, e), rhs=qtb(j, n, u, e),
+                        nc.tensor.matmul(out=tiles["sc%d%d" % (s, n // 4)][:, n % 4, :], lhsT=qtb(i, n, u, e), rhs=qtb(j, n, u, e),
                                          start=(u == 0 and e == 0), stop=(u == 3 and e == 1))
-                if s < 3:
-                    x_transpose_bank(s + 1, n, 6 + n % 2, "v" if (s == 0 and n % 2 == 1) else "s")
-                if 1 <= s <= 3 and n == 3:
-                    expo(s - 1)
+            return emit
 
-        def maxsub(s):
-            pair = sc[s]
-            pm = small.tile([P, 2, P], F32, name="pm", tag="pm")
-            for hh in range(2):
-                nc.vector.tensor_reduce(out=pm[:, hh, :], in_=pair[hh][:].rearrange("p h c -> p c h"),
-                                        axis=AX.X, op=ALU.max)
-            m = small.tile([P, P], F32, name="m", tag="m")
-            if MULT_G:
-                nc.vector.tensor_reduce(out=m[:], in_=pm[:].rearrange("p h c -> p c h"), axis=AX.X, op=ALU.max)
-            else:
-                nc.vector.tensor_tensor(out=m[:], in0=pm[:, 0, :], in1=pm[:, 1, :], op=ALU.max)
-            d = dpool.tile([P, H, P], F32, name="d", tag="d")
-            dts[s] = d
-            for hh in range(2):
-                nc.vector.tensor_tensor(out=d[:, 4 * hh:4 * (hh + 1), :], in0=pair[hh][:],
-                                        in1=m[:].unsqueeze(1).to_broadcast([P, 4, P]), op=ALU.subtract)
-
-        def fin(s):
-            i, j = BLOCKS[s]
-            d = dts[s]
-            t1 = small.tile([P, 4, P], F32, name="t1", tag="t1", bufs=1)
-            nc.vector.tensor_tensor(out=t1[:], in0=d[:, 0:4, :], in1=d[:, 4:8, :], op=ALU.add)
-            nc.vector.tensor_tensor(out=t1[:, 0:2, :], in0=t1[:, 0:2, :], in1=t1[:, 2:4, :], op=ALU.add)
-            z = small.tile([P, P], F32, name="z", tag="z")
-            nc.vector.tensor_tensor(out=z[:], in0=t1[:, 0, :], in1=t1[:, 1, :], op=ALU.add)
-            r = small.tile([P, P], F32, name="r", tag="r")
-            nc.vector.reciprocal(out=r[:], in_=z[:])
-            eng = nc.gpsimd if (MULT_G and s < NB - 1) else nc.vector
-            eng.tensor_tensor(out=rng[j][:, i, :, :], in0=d[:],
-                              in1=r[:].unsqueeze(1).to_broadcast([P, H, P]), op=ALU.mult)
-            store_block(i, j)
-
-        def mirror(s):
-            i, j = BLOCKS[s]
-            if i == j:
-                return
-            for hh in range(2):
-                tb = bank(6 + hh)
+        def mirror(name, s, hh, idx):
+            def emit(eng):
+                i, j = BLOCKS[s]
+                tb = bank(idx)
+                tiles[name] = tb
                 for nn in range(4):
                     nc.tensor.transpose(tb[:, nn, :], rng[j][:, i, 4 * hh + nn, :], ident[:])
-                nc.scalar.copy(out=rng[i][:, j, 4 * hh:4 * (hh + 1), :], in_=tb[:])
-            store_block(j, i)
+            return emit
 
-        gas = {}
-        acs = []
+        def copy_mirror(name, s, hh):
+            def emit(eng):
+                i, j = BLOCKS[s]
+                copy_on(eng, rng[i][:, j, 4 * hh:4 * (hh + 1), :], tiles[name][:])
+            return emit
 
-        def t4(j, k, eng):
-            ga = stage.tile([P, 2, P, 4], BF16, name="ga", tag="ga", align_bytes=64)
-            gas[(j, k)] = ga
-            copy_on(eng, ga[:].rearrange("p n (q i) t -> p (n q) t i", i=4),
-                    rng[j][:, :, 2 * k:2 * (k + 1), :].rearrange("p t n (q i) -> p (n q) t i", i=4))
-
-        def t5(j, k):
-            if not acs:
-                acs.append(big.tile([P, H, C], U32, name="ac", offset=80 * KIB, align_bytes=64))
-            ga = gas[(j, k)]
-            ac = acs[0]
-            for nn in range(2):
-                n = 2 * k + nn
-                nc.vector.quantize_mx(out=ac[:, n, P * j:P * (j + 1)].bitcast(FP8X4),
-                                      scales=asc[:, n, P * j:P * (j + 1)],
-                                      in_=ga[:, nn, :, :].rearrange("p c t -> p (c t)"))
-
-        gq_off = [64, 0, 16, 32]
-        gqp = {}
-
-        def regroup(q, eng):
-            n = q // 2
-            a = q % 2
-            hp = n // 2
-            if hp not in gqp:
-                gqp[hp] = big.tile([P, 2, 8, P, 4], BF16, name="gq%d" % hp, offset=gq_off[hp] * KIB, align_bytes=64)
-            base = WD * (n % 2) + 512 * a
-            src = xs[hp][:, :, base:base + 512].rearrange("p t (m i) -> p m t i", i=4)
-            dst = gqp[hp][:, n % 2, 4 * a:4 * (a + 1), :, :].rearrange("p i m t -> p m t i")
-            copy_on(eng, dst, src)
-
-        qcodes = {}
-
-        def quantise_q(n):
-            if n < 2:
-                codes = qc01[:, n, :]
-                scales = qs01[:, n, :]
-            else:
-                base = (64 + 5 * (n - 2)) if n < 5 else 5 * (n - 5)
-                qc_t = big.tile([P, WD], U32, name="qc%d" % n, offset=base * KIB, align_bytes=64)
-                qs_t = big.tile([P, WD], U8, name="qs%d" % n, offset=(base + 4) * KIB, align_bytes=64)
-                codes = qc_t[:]
-                scales = qs_t[:]
-            qcodes[n] = (codes, scales)
-            nc.vector.quantize_mx(out=codes.bitcast(FP8X4), scales=scales,
-                                  in_=gqp[n // 2][:, n % 2, :, :, :].rearrange("p r m t -> p (r m t)"))
-
-        for n in range(H):
-            x_transpose_bank(0, n, n, "v" if n % 2 == 1 else "s")
-
-        for s in range(NB + XLAG):
-            for j in range(2):
-                u = s - (7 + 2 * j)
-                if u == 0 or u == 1:
-                    t4(j, 2 * u, "s")
-                    t4(j, 2 * u + 1, "s")
-            if 4 <= s <= 9:
-                regroup(s - 4, "s")
-            if s < NB:
-                pe_scores(s)
-                maxsub(s)
-                if s >= 3:
-                    expo(s)
-            if s == 6 or s == 8:
-                quantise_q((s - 6) // 2)
-            if s == 8:
-                for k in range(4):
-                    t5(0, k)
-            if 1 <= s <= NB:
-                fin(s - 1)
-            if XLAG <= s:
-                mirror(s - XLAG)
-            if s == 10:
-                for k in range(4):
-                    t5(1, k)
-
-        def last_ranges(k):
-            t4(2, k, "s")
-            t4(3, k, "v")
-            t5(2, k)
-            t5(3, k)
-
-        h_off = [96, 104, 112, 120, 128, 136, 144, 152, 96, 104, 112, 120, 160, 168, 176, 184]
-        last_ranges(0)
-        for n in range(H):
-            codes, scales = qcodes[n]
-            ac = acs[0]
-            for a in range(2):
-                if n % 2 == 0 and a == 1 and n // 2 + 1 < 4:
-                    last_ranges(n // 2 + 1)
-                if 3 <= n + 2 < H:
-                    regroup(2 * (n + 2) + a, "v")
-                hsb = big.tile([P, 4, C], F32, name="h%d_%d" % (n, a), offset=h_off[2 * n + a] * KIB, align_bytes=64)
-                for rr in range(4):
-                    r8 = 4 * a + rr
-                    bk = bank(r8)
-                    flat = bk[:].rearrange("p a b -> p (a b)")
-                    nc.tensor.matmul_mx(out=flat,
-                                        lhsT=codes[:, P * r8:P * (r8 + 1)].bitcast(FP8X4),
-                                        lhsT_scale=scales[:, P * r8:P * (r8 + 1)],
-                                        rhs=ac[:, n, :].bitcast(FP8X4),
-                                        rhs_scale=asc[:, n, :],
+        def mx(name, n, grp, b, idx):
+            def emit(eng):
+                j0, width = GROUPS[grp]
+                per = 512 // width
+                bk = bank(idx)
+                tiles[name] = bk
+                flat = bk[:].rearrange("p a b -> p (a b)")
+                codes, scales = tiles["q%d" % n]
+                for q in range(per):
+                    w8 = per * b + q
+                    nc.tensor.matmul_mx(out=flat[:, width * q:width * (q + 1)],
+                                        lhsT=codes[:, P * w8:P * (w8 + 1)].bitcast(FP8X4),
+                                        lhsT_scale=scales[:, P * w8:P * (w8 + 1)],
+                                        rhs=tiles["ac"][:, n, P * j0:P * j0 + width].bitcast(FP8X4),
+                                        rhs_scale=asc[:, n, P * j0:P * j0 + width],
                                         start=True, stop=True)
-                    if n + 2 >= H:
-                        eng = "v" if rr % 2 == 1 else "s"
-                    else:
-                        eng = "v" if (rr == 3 and a == 1) else "s"
-                    copy_on(eng, hsb[:, rr, :], flat)
-                hv = h2[WD * n + 512 * a:WD * n + 512 * (a + 1), :].rearrange("(m r) c -> m r c", r=4)
-                nc.sync.dma_start(out=hv, in_=hsb[:])
-            if n + 2 < H:
-                quantise_q(n + 2)
+            return emit
+
+        def copy_h(name, key, slot, half):
+            def emit(eng):
+                if key not in tiles:
+                    tiles[key] = big.tile([P, 2, 512], F32, name=key, offset=H_OFF[slot] * KIB, align_bytes=64)
+                copy_on(eng, tiles[key][:, half, :], tiles[name][:].rearrange("p a b -> p (a b)"))
+            return emit
+
+        def store_h(key, n, grp, b):
+            def emit(eng):
+                j0, width = GROUPS[grp]
+                per = 512 // width
+                r0 = WD * n + P * per * b
+                nc.sync.dma_start(out=h2[r0:r0 + 2 * per * P, P * j0:P * j0 + width].rearrange("(q p) c -> p q c", p=P),
+                                  in_=tiles[key][:].rearrange("p x (y c) -> p (x y) c", c=width))
+            return emit
+
+        def smax(s, hh):
+            def emit(eng):
+                if hh == 0:
+                    tiles["pm%d" % s] = small.tile([P, 2, P], F32, name="pm", tag="pm")
+                nc.vector.tensor_reduce(out=tiles["pm%d" % s][:, hh, :], in_=tiles["sc%d%d" % (s, hh)][:].rearrange("p h c -> p c h"),
+                                        axis=AX.X, op=ALU.max)
+            return emit
+
+        def smax2(s):
+            def emit(eng):
+                m = small.tile([P, P], F32, name="m%d" % (s % 2), tag="m%d" % (s % 2))
+                tiles["m%d" % s] = m
+                nc.vector.tensor_reduce(out=m[:], in_=tiles["pm%d" % s][:].rearrange("p h c -> p c h"), axis=AX.X, op=ALU.max)
+            return emit
+
+        def sub(s, hh, slot):
+            def emit(eng):
+                if hh == 0:
+                    tiles["d%d" % s] = stage.tile([P, H, P], F32, name="d%d" % slot, tag="d%d" % slot)
+                nc.vector.tensor_tensor(out=tiles["d%d" % s][:, 4 * hh:4 * (hh + 1), :], in0=tiles["sc%d%d" % (s, hh)][:],
+                                        in1=tiles["m%d" % s][:].unsqueeze(1).to_broadcast([P, 4, P]), op=ALU.subtract)
+            return emit
+
+        def expo(s):
+            def emit(eng):
+                d = tiles["d%d" % s]
+                nc.scalar.activation(out=d[:], in_=d[:], func=ACT.Exp, scale=rg[:, 0:1])
+            return emit
+
+        def new_z(s):
+            tiles["z%d" % s] = small.tile([P, P], F32, name="z%d" % (s % 2), tag="z%d" % (s % 2))
+            return tiles["z%d" % s]
+
+        def red(s, k):
+            def emit(eng):
+                if k == 0:
+                    tiles["tf%d" % s] = small.tile([P, 2, P], F32, name="tf", tag="tf")
+                tf = tiles["tf%d" % s]
+                if k < 2:
+                    nc.vector.tensor_reduce(out=tf[:, k, :], in_=tiles["d%d" % s][:, 4 * k:4 * (k + 1), :].rearrange("p h c -> p c h"),
+                                            axis=AX.X, op=ALU.add)
+                else:
+                    nc.vector.tensor_reduce(out=new_z(s)[:], in_=tf[:].rearrange("p h c -> p c h"), axis=AX.X, op=ALU.add)
+            return emit
+
+        def add(s, k):
+            def emit(eng):
+                e = nc.gpsimd if eng == "g" else nc.vector
+                if k == 0:
+                    tiles["t%d" % s] = small.tile([P, 4, P], F32, name="t1", tag="t1")
+                t1 = tiles["t%d" % s]
+                if k == 0:
+                    d = tiles["d%d" % s]
+                    e.tensor_tensor(out=t1[:], in0=d[:, 0:4, :], in1=d[:, 4:8, :], op=ALU.add)
+                elif k == 1:
+                    e.tensor_tensor(out=t1[:, 0:2, :], in0=t1[:, 0:2, :], in1=t1[:, 2:4, :], op=ALU.add)
+                else:
+                    e.tensor_tensor(out=new_z(s)[:], in0=t1[:, 0, :], in1=t1[:, 1, :], op=ALU.add)
+            return emit
+
+        def recip(s):
+            def emit(eng):
+                r = small.tile([P, P], F32, name="r%d" % (s % 2), tag="r%d" % (s % 2))
+                tiles["r%d" % s] = r
+                nc.vector.reciprocal(out=r[:], in_=tiles["z%d" % s][:])
+            return emit
+
+        def mult(s):
+            def emit(eng):
+                i, j = BLOCKS[s]
+                e = nc.gpsimd if eng == "g" else nc.vector
+                e.tensor_tensor(out=rng[j][:, i, :, :], in0=tiles["d%d" % s][:],
+                                in1=tiles["r%d" % s][:].unsqueeze(1).to_broadcast([P, H, P]), op=ALU.mult)
+            return emit
+
+        def store_attn(a, b):
+            def emit(eng):
+                nc.sync.dma_start(out=attn3[:, P * a:P * (a + 1), P * b:P * (b + 1)].rearrange("n p c -> p n c"), in_=rng[b][:, a, :, :])
+            return emit
+
+        def regroup_a(j, k, slot):
+            def emit(eng):
+                ga = stage.tile([P, 2, P, 4], BF16, name="ga%d" % slot, tag="ga%d" % slot, align_bytes=64)
+                tiles["ga%d%d" % (j, k)] = ga
+                src = rng[j][:, :, 2 * k:2 * (k + 1), :]
+                if eng == "g":
+                    nc.gpsimd.tensor_scalar(out=ga[:].rearrange("p n c t -> p (n c) t"), in0=src.rearrange("p t n c -> p (n c) t"),
+                                            scalar1=1.0, scalar2=0.0, op0=ALU.mult, op1=ALU.add)
+                else:
+                    copy_on(eng, ga[:].rearrange("p n (q i) t -> p (n q) t i", i=4), src.rearrange("p t n (q i) -> p (n q) t i", i=4))
+            return emit
+
+        def quant_a(j, k):
+            def emit(eng):
+                if "ac" not in tiles:
+                    tiles["ac"] = big.tile([P, H, C], U32, name="ac", offset=64 * KIB, align_bytes=64)
+                for nn in range(2):
+                    n = 2 * k + nn
+                    nc.vector.quantize_mx(out=tiles["ac"][:, n, P * j:P * (j + 1)].bitcast(FP8X4), scales=asc[:, n, P * j:P * (j + 1)],
+                                          in_=tiles["ga%d%d" % (j, k)][:, nn, :, :].rearrange("p c t -> p (c t)"))
+            return emit
+
+        def regroup_q(n, a):
+            def emit(eng):
+                key = "gq%d" % n
+                if key not in tiles:
+                    tiles[key] = stage.tile([P, WD, 4], BF16, name="gq%d" % (n % 2), tag="gq%d" % (n % 2), align_bytes=64)
+                base = WD * (n % 2) + 512 * a
+                src = xs[n // 2][:, :, base:base + 512]
+                dst = tiles[key][:, 512 * a:512 * (a + 1), :]
+                if eng == "g":
+                    nc.gpsimd.tensor_scalar(out=dst, in0=src.rearrange("p t m -> p m t"), scalar1=1.0, scalar2=0.0, op0=ALU.mult, op1=ALU.add)
+                else:
+                    copy_on(eng, dst.rearrange("p (m i) t -> p m t i", i=4), src.rearrange("p t (m i) -> p m t i", i=4))
+            return emit
+
+        def quant_q(n):
+            def emit(eng):
+                codes = big.tile([P, WD], U32, name="qc%d" % n, offset=CODE_OFF[n] * KIB, align_bytes=64)
+                scales = big.tile([P, WD], U8, name="qs%d" % n, offset=(CODE_OFF[n] + 4) * KIB, align_bytes=64)
+                tiles["q%d" % n] = (codes, scales)
+                nc.vector.quantize_mx(out=codes[:].bitcast(FP8X4), scales=scales[:], in_=tiles["gq%d" % n][:].rearrange("p w t -> p (w t)"))
+            return emit
+
+        freed = {}
+        late = 0
+        slots = {}
+        for name in prog["t"]:
+            k = name[0]
+            a = [int(ch) for ch in name[1:]]
+            if k == "T":
+                idx = a[1] if a[0] == 0 else 6 + a[1] % 2
+                ops[name] = ([freed[idx]] if idx in freed else [], transpose_x(name, a[0], a[1], idx))
+                ops["c" + name] = ([name], copy_x(name, a[0], a[1]))
+                freed[idx] = "c" + name
+            elif k == "S":
+                i, j = BLOCKS[a[0]]
+                idx = 2 * (a[0] % 3) + a[1] // 4
+                ops[name] = (["cT%d%d" % (i, a[1]), "cT%d%d" % (j, a[1])] + ([freed[idx]] if idx in freed else []), score(a[0], a[1], idx))
+                if a[1] % 4 == 3:
+                    freed[idx] = "B%d%d" % (a[0], a[1] // 4)
+            elif k == "M":
+                idx = 6 + a[1]
+                ops[name] = (["U%d" % a[0], freed[idx]], mirror(name, a[0], a[1], idx))
+                ops["c" + name] = ([name], copy_mirror(name, a[0], a[1]))
+                freed[idx] = "c" + name
+            else:
+                n, grp, b = a
+                idx = LATE[late] if late < len(LATE) else ROTATE[(late - len(LATE)) % 8]
+                late += 1
+                j0, width = GROUPS[grp]
+                ops[name] = (["Q%d" % n, freed[idx]] + ["Z%d%d" % (j, n // 2) for j in range(j0, j0 + width // P)], mx(name, n, grp, b, idx))
+                freed[idx] = "c" + name
+                key = "h%d%d%d" % (n, grp, b // 2)
+                if key not in slots:
+                    slots[key] = len(slots)
+                need = [name]
+                if slots[key] >= len(H_OFF):
+                    need.append([o for o in slots if slots[o] == slots[key] - len(H_OFF)][0])
+                ops["c" + name] = (need, copy_h(name, key, slots[key] % len(H_OFF), b % 2))
+                if b % 2 == 1:
+                    ops[key] = (["cH%d%d%d" % (n, grp, b - 1), "cH%d%d%d" % (n, grp, b)], store_h(key, n, grp, b - 1))
+        dord = [int(name[1]) for name in prog["v"] if name[0] == "B" and name[2] == "0"]
+        zord = [name[1:] for name in prog["v"] if name[0] == "Z"]
+        for s in range(NB):
+            i, j = BLOCKS[s]
+            for hh in range(2):
+                ops["A%d%d" % (s, hh)] = (["S%d%d" % (s, 4 * hh + q) for q in range(4)], smax(s, hh))
+                p = dord.index(s)
+                ops["B%d%d" % (s, hh)] = (["X%d" % s] + (["U%d" % dord[p - 3]] if p >= 3 else []), sub(s, hh, p % 3))
+            ops["X%d" % s] = (["A%d0" % s, "A%d1" % s], smax2(s))
+            ops["E%d" % s] = (["B%d0" % s, "B%d1" % s], expo(s))
+            zfree = ["R%d" % (s - 2)] if s >= 2 else []
+            for k in range(3):
+                ops["F%d%d" % (s, k)] = (["E%d" % s] + (zfree + ["F%d0" % s, "F%d1" % s] if k == 2 else []), red(s, k))
+                for c in "DG":
+                    ops["%s%d%d" % (c, s, k)] = ((["E%d" % s] if k == 0 else ["%s%d%d" % (c, s, k - 1)]) + (zfree if k == 2 else []), add(s, k))
+            last = [c for c in ("F%d2" % s, "D%d2" % s, "G%d2" % s) if c in where][0]
+            ops["R%d" % s] = ([last] + (["U%d" % (s - 2)] if s >= 2 else []), recip(s))
+            ops["U%d" % s] = (["R%d" % s], mult(s))
+            ops["a%d" % s] = (["U%d" % s], store_attn(i, j))
+            ops["b%d" % s] = (["cM%d0" % s, "cM%d1" % s], store_attn(j, i))
+        ops["D80"] = (["E8", "G72"], add(8, 0))
+        for p in range(len(zord)):
+            j, k = int(zord[p][0]), int(zord[p][1])
+            need = ["Z" + zord[p - 4]] if p >= 4 else ["S37"]
+            for i in range(T):
+                if (i, j) in BLOCKS:
+                    need.append("U%d" % BLOCKS.index((i, j)))
+                else:
+                    need.append("cM%d%d" % (BLOCKS.index((j, i)), k // 2))
+            ops["P" + zord[p]] = (need, regroup_a(j, k, p % 4))
+            ops["Z" + zord[p]] = (["P" + zord[p]], quant_a(j, k))
+        for n in range(H):
+            for a in range(2):
+                ops["K%d" % (2 * n + a)] = (["Q%d" % (n - 2)] if n >= 2 else [], regroup_q(n, a))
+            first = 0 if n < 3 else 4 if n < 6 else 8
+            ops["Q%d" % n] = (["T3%d" % (first // 2), "T3%d" % (first // 2 + 1), "K%d" % (2 * n), "K%d" % (2 * n + 1)] + ["K%d" % q for q in range(first, first + 4)], quant_q(n))
+
+        done = {}
+        pos = {e: 0 for e in prog}
+        total = len(where)
+        while len(done) < total:
+            before = len(done)
+            for e in prog:
+                while pos[e] < len(prog[e]) and all(o in done for o in ops[prog[e][pos[e]]][0]):
+                    name = prog[e][pos[e]]
+                    ops[name][1](e)
+                    done[name] = True
+                    pos[e] += 1
+            assert len(done) > before, ["%s" % prog[e][pos[e]] for e in prog if pos[e] < len(prog[e])]

@@ -54,6 +54,10 @@ def cb(n, bs=(0, 2)):
     return ["cH%d1%d" % (n, b) for b in bs]
 
 
+def red(s):
+    return ["F%d0" % s, "F%d1" % s, "F%d2" % s]
+
+
 def scores(s):
     return ["S%d%d" % (s, n) for n in R8]
 
@@ -61,8 +65,8 @@ def scores(s):
 def programs():
     t = ['T0%d' % n for n in R8]
     for b, u in ((0, 1), (1, 2), (2, 3)):
-        for n in R8:
-            t += ['S%d%d' % (b, n), 'T%d%d' % (u, n)]
+        for n in (0, 2, 4, 6):
+            t += ['S%d%d' % (b, n), 'S%d%d' % (b, n + 1), 'T%d%d' % (u, n), 'T%d%d' % (u, n + 1)]
     for b in (3, 4, 5):
         t += scores(b)
     t += ['M10', 'M11'] + scores(6) + ['M20', 'M21'] + scores(7) + ['M30', 'M31'] + scores(8) + scores(9)
@@ -70,17 +74,20 @@ def programs():
     hb = [['H%d1%d' % (n, b) for b in R4] for n in R8]
     t += ha[0] + ha[1] + ha[2] + ['M50', 'M51', 'M60', 'M61'] + ha[3] + ['M80', 'M81'] + ha[4] + hb[0] + hb[1] + hb[2] + hb[3] + ha[5] + ha[6] + hb[4] + hb[5] + ha[7] + hb[6] + hb[7]
     v = ['cT01', 'cT03', 'cT05', 'cT07', 'cT11', 'cT13', 'cT15', 'A00', 'cT17', 'A01', 'X0', 'B00', 'B01', 'A10', 'A11', 'X1', 'B10', 'B11', 'Q0', 'cT33', 'A20', 'cT35', 'A21', 'R0', 'X2', 'cT37', 'B20', 'B21', 'Q1']
+    vector_sums = [3,5]
     for b in (3, 4, 5, 6):
-        v += ['A%d0' % b, 'A%d1' % b, 'R%d' % (b - 2), 'X%d' % b, 'B%d0' % b, 'B%d1' % b]
+        v += ['A%d0' % b, 'A%d1' % b] + (['R%d' % (b - 2)] if b - 2 not in vector_sums else []) + ['X%d' % b, 'B%d0' % b, 'B%d1' % b]
+        if b - 1 in vector_sums:
+            v += red(b - 1)[:2] + red(b - 1)[2:] + ['R%d' % (b - 1)]
         if b == 4:
             v += ['Q2']
-    v += ['A70', 'A71', 'F60', 'F61', 'Z00', 'R5', 'F62', 'X7', 'A80', 'R6', 'A81', 'U6', 'X8', 'B70', 'Z01', 'B71', 'Z02', 'A90', 'Z03', 'Z10', 'B80', 'A91', 'B81', 'X9', 'R7', 'Z11', 'B90', 'B91']
+    v += ['A70', 'A71', 'F60', 'F61', 'Z00', 'F62', 'X7', 'A80', 'R6', 'A81', 'U6', 'X8', 'B70', 'Z01', 'B71', 'Z02', 'A90', 'Z03', 'Z10', 'B80', 'A91', 'B81', 'X9', 'R7', 'Z11', 'B90', 'B91']
     v += tree(8) + ['R8', 'Q3', 'cH203', 'K8', 'D90', 'U8', 'D91', 'Z12', 'D92', 'K9', 'R9', 'Q4', 'U9', 'cH303', 'Z13', 'cH403', 'Z20', 'Z30']
     v += ['cH011', 'cH013', 'K10', 'cH111', 'cH113', 'Z21', 'Z31', 'K11', 'Q5', 'cH211', 'cH213', 'K12', 'cH311', 'cH313', 'K13', 'Q6', 'cH503', 'Z22', 'Z32', 'K14', 'cH603', 'K15', 'Q7', 'cH411', 'cH413', 'cH511', 'cH513', 'cH703', 'Z23', 'Z33', 'cH611', 'cH613', 'cH711', 'cH713']
     s = ['cT00', 'cT02', 'cT04', 'cT06', 'cT10', 'cT12', 'cT14', 'cT16', 'cT20', 'cT21', 'cT22', 'cT23', 'E0', 'cT24', 'cT25', 'cT26', 'cT27', 'cT30', 'cT31', 'E1', 'cT32', 'cT34', 'cT36', 'K4', 'E2']
     s += ['K5', 'E3', 'K6', 'E4', 'cM10', 'cM11', 'K7', 'E5', 'cM20', 'cM21', 'P00', 'E6', 'P01', 'P02', 'P03', 'cM30', 'cM31', 'P10', 'E7', 'P11']
     s += ca(0) + ['E8'] + ca(1) + ['E9', 'P12'] + ca(2, range(3)) + ['cM50', 'cM51', 'P13', 'cM60', 'cM61'] + ca(3, range(3)) + ['cM80', 'cM81', 'P30'] + ca(4, range(3)) + ['P31'] + cb(0) + cb(1) + cb(2) + cb(3) + ['P32'] + ca(5, range(3)) + ca(6, range(3)) + ['P33'] + cb(4) + cb(5) + ca(7, range(3)) + cb(6) + cb(7)
-    g = ['K0', 'K1', 'K2', 'K3'] + gsum(0) + gsum(1) + ['U0'] + gsum(2) + ['U1'] + gsum(3) + ['U2'] + gsum(4) + ['U3'] + gsum(5) + ['U4', 'U5'] + gsum(7) + ['U7', 'P20', 'P21', 'P22', 'P23']
+    g = ['K0', 'K1', 'K2', 'K3'] + gsum(0) + gsum(1) + ['U0'] + gsum(2) + ['U1'] + ['U2'] + gsum(4) + ['U3'] + ['U4', 'U5'] + gsum(7) + ['U7', 'P20', 'P21', 'P22', 'P23']
     q = ["a0", "a1", "b1", "a2", "b2", "a3", "a4", "b3", "a5", "a6", "h000", "h001", "h100", "h101", "a7", "h200", "h201", "b5", "a8", "b6", "h300", "h301", "b8", "a9"]
     q += ["h%d%d%d" % (n, grp, x) for n, grp in ((4, 0), (0, 1), (1, 1), (2, 1), (3, 1), (5, 0), (6, 0), (4, 1), (5, 1), (7, 0), (6, 1), (7, 1)) for x in range(2)]
     return {"t": t, "v": v, "s": s, "g": g, "q": q}

@@ -74,20 +74,18 @@ def programs():
     hb = [['H%d1%d' % (n, b) for b in R4] for n in R8]
     t += ha[0] + ha[1] + ha[2] + ['M50', 'M51', 'M60', 'M61'] + ha[3] + ['M80', 'M81'] + ha[4] + hb[0] + hb[1] + hb[2] + hb[3] + ha[5] + ha[6] + hb[4] + hb[5] + ha[7] + hb[6] + hb[7]
     v = ['cT01', 'cT03', 'cT05', 'cT07', 'cT11', 'cT13', 'cT15', 'A00', 'cT17', 'A01', 'X0', 'B00', 'B01', 'A10', 'A11', 'X1', 'B10', 'B11', 'Q0', 'cT33', 'A20', 'cT35', 'A21', 'R0', 'X2', 'cT37', 'B20', 'B21', 'Q1']
-    vector_sums = [3,5]
+    vector_sums = [3]
     for b in (3, 4, 5, 6):
         v += ['A%d0' % b, 'A%d1' % b] + (['R%d' % (b - 2)] if b - 2 not in vector_sums else []) + ['X%d' % b, 'B%d0' % b, 'B%d1' % b]
         if b - 1 in vector_sums:
             v += red(b - 1)[:2] + red(b - 1)[2:] + ['R%d' % (b - 1)]
-        if b == 4:
-            v += ['Q2']
-    v += ['A70', 'A71', 'F60', 'F61', 'Z00', 'F62', 'X7', 'A80', 'R6', 'A81', 'U6', 'X8', 'B70', 'Z01', 'B71', 'Z02', 'A90', 'Z03', 'Z10', 'B80', 'A91', 'B81', 'X9', 'R7', 'Z11', 'B90', 'B91']
-    v += tree(8) + ['R8', 'Q3', 'cH203', 'K8', 'D90', 'U8', 'D91', 'Z12', 'D92', 'K9', 'R9', 'Q4', 'U9', 'cH303', 'Z13', 'cH403', 'Z20', 'Z30']
-    v += ['cH011', 'cH013', 'K10', 'cH111', 'cH113', 'Z21', 'Z31', 'K11', 'Q5', 'cH211', 'cH213', 'K12', 'cH311', 'cH313', 'K13', 'Q6', 'cH503', 'Z22', 'Z32', 'K14', 'cH603', 'K15', 'Q7', 'cH411', 'cH413', 'cH511', 'cH513', 'cH703', 'Z23', 'Z33', 'cH611', 'cH613', 'cH711', 'cH713']
+    v += ['F50', 'F51', 'A70', 'F52', 'F60', 'R5', 'F61', 'A71', 'F62', 'X7', 'R6', 'B70', 'U6', 'B71', 'Z00', 'Z01', 'A80', 'Z02', 'A81', 'Z03', 'X8', 'Z10', 'Q2', 'A90', 'B80', 'A91', 'B81', 'X9', 'R7', 'Z11', 'B90', 'B91']
+    v += ['Q3', 'D80', 'K8', 'D81', 'D82', 'D90', 'R8', 'D91', 'U8', 'D92', 'Z12', 'R9', 'K9', 'U9', 'Q4', 'K10', 'Z13', 'K11', 'Z20', 'Z30', 'Q5']
+    v += ['cH011', 'cH013', 'cH111', 'cH113', 'Z21', 'Z31', 'cH211', 'cH213', 'K12', 'cH311', 'cH313', 'K13', 'Q6', 'cH503', 'P22', 'K14', 'Z22', 'Z32', 'cH603', 'cH411', 'cH413', 'K15', 'Q7', 'cH511', 'cH513', 'P23', 'cH703', 'Z23', 'Z33', 'cH611', 'cH613', 'cH711', 'cH713']
     s = ['cT00', 'cT02', 'cT04', 'cT06', 'cT10', 'cT12', 'cT14', 'cT16', 'cT20', 'cT21', 'cT22', 'cT23', 'E0', 'cT24', 'cT25', 'cT26', 'cT27', 'cT30', 'cT31', 'E1', 'cT32', 'cT34', 'cT36', 'K4', 'E2']
     s += ['K5', 'E3', 'K6', 'E4', 'cM10', 'cM11', 'K7', 'E5', 'cM20', 'cM21', 'P00', 'E6', 'P01', 'P02', 'P03', 'cM30', 'cM31', 'P10', 'E7', 'P11']
-    s += ca(0) + ['E8'] + ca(1) + ['E9', 'P12'] + ca(2, range(3)) + ['cM50', 'cM51', 'P13', 'cM60', 'cM61'] + ca(3, range(3)) + ['cM80', 'cM81', 'P30'] + ca(4, range(3)) + ['P31'] + cb(0) + cb(1) + cb(2) + cb(3) + ['P32'] + ca(5, range(3)) + ca(6, range(3)) + ['P33'] + cb(4) + cb(5) + ca(7, range(3)) + cb(6) + cb(7)
-    g = ['K0', 'K1', 'K2', 'K3'] + gsum(0) + gsum(1) + ['U0'] + gsum(2) + ['U1'] + ['U2'] + gsum(4) + ['U3'] + ['U4', 'U5'] + gsum(7) + ['U7', 'P20', 'P21', 'P22', 'P23']
+    s += ca(0) + ['E8'] + ca(1) + ['E9', 'P12'] + ca(2) + ['cM50', 'cM51', 'P13', 'cM60', 'cM61'] + ca(3) + ['cM80', 'cM81', 'P30'] + ca(4) + ['P31'] + cb(0) + cb(1) + cb(2) + cb(3) + ['P32'] + ca(5, range(3)) + ca(6, range(3)) + ['P33'] + cb(4) + cb(5) + ca(7, range(3)) + cb(6) + cb(7)
+    g = ['K0', 'K1', 'K2', 'K3'] + gsum(0) + gsum(1) + ['U0'] + gsum(2) + ['U1'] + ['U2'] + gsum(4) + ['U3'] + ['U4', 'U5'] + gsum(7) + ['U7', 'P20', 'P21']
     q = ["a0", "a1", "b1", "a2", "b2", "a3", "a4", "b3", "a5", "a6", "h000", "h001", "h100", "h101", "a7", "h200", "h201", "b5", "a8", "b6", "h300", "h301", "b8", "a9"]
     q += ["h%d%d%d" % (n, grp, x) for n, grp in ((4, 0), (0, 1), (1, 1), (2, 1), (3, 1), (5, 0), (6, 0), (4, 1), (5, 1), (7, 0), (6, 1), (7, 1)) for x in range(2)]
     return {"t": t, "v": v, "s": s, "g": g, "q": q}

@@ -54,39 +54,39 @@ def cb(n, bs=(0, 2)):
     return ["cH%d1%d" % (n, b) for b in bs]
 
 
-def red(s):
-    return ["F%d0" % s, "F%d1" % s, "F%d2" % s]
-
-
 def scores(s):
     return ["S%d%d" % (s, n) for n in R8]
 
 
 def programs():
-    t = ['T0%d' % n for n in R8]
-    for b, u in ((0, 1), (1, 2), (2, 3)):
+    t = ['T00', 'T01']
+    for n in (2, 4, 6):
+        t += ['T0%d' % n, 'T0%d' % (n + 1), 'S0%d' % (n - 2), 'S0%d' % (n - 1)]
+    t += ['T10', 'T11', 'S06', 'S07'] + ['T1%d' % n for n in range(2, 8)]
+    for b, u in ((1, 2), (2, 3)):
         for n in (0, 2, 4, 6):
             t += ['S%d%d' % (b, n), 'S%d%d' % (b, n + 1), 'T%d%d' % (u, n), 'T%d%d' % (u, n + 1)]
     for b in (3, 4, 5):
         t += scores(b)
-    t += ['M10', 'M11'] + scores(6) + ['M20', 'M21'] + scores(7) + ['M30', 'M31'] + scores(8) + scores(9)
+    t += ['M10', 'M11'] + scores(6) + ['M20', 'M21'] + scores(7) + ['M30', 'M31'] + scores(8) + ['M50', 'M51'] + scores(9)
     ha = [['H%d0%d' % (n, b) for b in R4] for n in R8]
     hb = [['H%d1%d' % (n, b) for b in R4] for n in R8]
-    t += ha[0] + ha[1] + ha[2] + ['M50', 'M51', 'M60', 'M61'] + ha[3] + ['M80', 'M81'] + ha[4] + hb[0] + hb[1] + hb[2] + hb[3] + ha[5] + ha[6] + hb[4] + hb[5] + ha[7] + hb[6] + hb[7]
-    v = ['cT01', 'cT03', 'cT05', 'cT07', 'cT11', 'cT13', 'cT15', 'A00', 'cT17', 'A01', 'X0', 'B00', 'B01', 'A10', 'A11', 'X1', 'B10', 'B11', 'Q0', 'cT33', 'A20', 'cT35', 'A21', 'R0', 'X2', 'cT37', 'B20', 'B21', 'Q1']
+    t += ha[0] + ha[1] + ha[2] + ['M60', 'M61'] + ha[3] + ['M80', 'M81'] + ha[4] + hb[0] + hb[1] + hb[2] + hb[3] + ha[5] + ha[6] + hb[4] + hb[5] + ha[7] + hb[6] + hb[7]
+    v = ['cT01', 'cT03', 'cT05', 'cT07', 'A00', 'cT11', 'A01', 'cT13', 'X0', 'cT15', 'B00', 'B01', 'cT17', 'K2', 'A10', 'K3', 'A11', 'X1', 'B10', 'B11', 'Q0', 'cT33', 'A20', 'cT35', 'A21', 'R0', 'X2', 'cT37', 'B20', 'B21', 'Q1']
     vector_sums = [3]
-    for b in (3, 4, 5, 6):
-        v += ['A%d0' % b, 'A%d1' % b] + (['R%d' % (b - 2)] if b - 2 not in vector_sums else []) + ['X%d' % b, 'B%d0' % b, 'B%d1' % b]
+    for b in (3, 4, 5):
+        v += ['A%d0' % b] + (['R%d' % (b - 2)] if b - 2 not in vector_sums else []) + ['A%d1' % b, 'X%d' % b, 'B%d0' % b, 'B%d1' % b]
         if b - 1 in vector_sums:
-            v += red(b - 1)[:2] + red(b - 1)[2:] + ['R%d' % (b - 1)]
-    v += ['F50', 'F51', 'A70', 'F52', 'F60', 'R5', 'F61', 'A71', 'F62', 'X7', 'R6', 'B70', 'U6', 'B71', 'Z00', 'Z01', 'A80', 'Z02', 'A81', 'Z03', 'X8', 'Z10', 'Q2', 'A90', 'B80', 'A91', 'B81', 'X9', 'R7', 'Z11', 'B90', 'B91']
-    v += ['Q3', 'D80', 'K8', 'D81', 'D82', 'D90', 'R8', 'D91', 'U8', 'D92', 'Z12', 'R9', 'K9', 'U9', 'Q4', 'K10', 'Z13', 'K11', 'Z20', 'Z30', 'Q5']
+            v += tree(b - 1) + ['R%d' % (b - 1)]
+    v += ['A60', 'R4', 'Q2', 'A61', 'X6', 'B60', 'B61']
+    v += ['D50', 'D60', 'D51', 'D61', 'D52', 'A70', 'R5', 'D62', 'A71', 'R6', 'X7', 'U6', 'B70', 'B71', 'Z00', 'Z01', 'A80', 'Z02', 'A81', 'Z03', 'X8', 'Z10', 'A90', 'B80', 'A91', 'B81', 'X9', 'R7', 'Z11', 'B90', 'B91']
+    v += ['Q3', 'D80', 'D81', 'D82', 'D90', 'R8', 'D91', 'U8', 'D92', 'Z12', 'R9', 'U9', 'Q4', 'K10', 'Z13', 'K11', 'Z20', 'Z30', 'Q5']
     v += ['cH011', 'cH013', 'cH111', 'cH113', 'Z21', 'Z31', 'cH211', 'cH213', 'K12', 'cH311', 'cH313', 'K13', 'Q6', 'cH503', 'P22', 'K14', 'Z22', 'Z32', 'cH603', 'cH411', 'cH413', 'K15', 'Q7', 'cH511', 'cH513', 'P23', 'cH703', 'Z23', 'Z33', 'cH611', 'cH613', 'cH711', 'cH713']
-    s = ['cT00', 'cT02', 'cT04', 'cT06', 'cT10', 'cT12', 'cT14', 'cT16', 'cT20', 'cT21', 'cT22', 'cT23', 'E0', 'cT24', 'cT25', 'cT26', 'cT27', 'cT30', 'cT31', 'E1', 'cT32', 'cT34', 'cT36', 'K4', 'E2']
-    s += ['K5', 'E3', 'K6', 'E4', 'cM10', 'cM11', 'K7', 'E5', 'cM20', 'cM21', 'P00', 'E6', 'P01', 'P02', 'P03', 'cM30', 'cM31', 'P10', 'E7', 'P11']
-    s += ca(0) + ['E8'] + ca(1) + ['E9', 'P12'] + ca(2) + ['cM50', 'cM51', 'P13', 'cM60', 'cM61'] + ca(3) + ['cM80', 'cM81', 'P30'] + ca(4) + ['P31'] + cb(0) + cb(1) + cb(2) + cb(3) + ['P32'] + ca(5, range(3)) + ca(6, range(3)) + ['P33'] + cb(4) + cb(5) + ca(7, range(3)) + cb(6) + cb(7)
-    g = ['K0', 'K1', 'K2', 'K3'] + gsum(0) + gsum(1) + ['U0'] + gsum(2) + ['U1'] + ['U2'] + gsum(4) + ['U3'] + ['U4', 'U5'] + gsum(7) + ['U7', 'P20', 'P21']
-    q = ["a0", "a1", "b1", "a2", "b2", "a3", "a4", "b3", "a5", "a6", "h000", "h001", "h100", "h101", "a7", "h200", "h201", "b5", "a8", "b6", "h300", "h301", "b8", "a9"]
+    s = ['cT00', 'cT02', 'cT04', 'cT06', 'cT10', 'cT12', 'cT14', 'cT16', 'E0', 'cT20', 'cT21', 'cT22', 'cT23', 'cT24', 'cT25', 'cT26', 'cT27', 'cT30', 'cT31', 'E1', 'cT32', 'cT34', 'cT36', 'K4', 'E2']
+    s += ['K5', 'E3', 'K6', 'E4', 'cM10', 'cM11', 'K7', 'E5', 'cM20', 'cM21', 'P00', 'E6', 'P01', 'P02', 'P03', 'cM30', 'cM31', 'K8', 'K9', 'cM50', 'cM51', 'P10', 'E7', 'P11']
+    s += ca(0) + ['E8'] + ca(1) + ['E9', 'P12'] + ca(2) + ['P13', 'cM60', 'cM61'] + ca(3) + ['cM80', 'cM81', 'P30'] + ca(4) + ['P31'] + cb(0) + cb(1) + cb(2) + cb(3) + ['P32'] + ca(5, range(3)) + ca(6, range(3)) + ['P33'] + cb(4) + cb(5) + ca(7, range(3)) + cb(6) + cb(7)
+    g = ['K0', 'K1'] + gsum(0) + gsum(1) + ['U0'] + gsum(2) + ['U1'] + ['U2'] + gsum(4) + ['U3'] + ['U4', 'U5'] + gsum(7) + ['U7', 'P20', 'P21']
+    q = ["a0", "a1", "b1", "a2", "b2", "a3", "a4", "b3", "a5", "a6", "b5", "h000", "h001", "h100", "h101", "a7", "h200", "h201", "a8", "b6", "h300", "h301", "b8", "a9"]
     q += ["h%d%d%d" % (n, grp, x) for n, grp in ((4, 0), (0, 1), (1, 1), (2, 1), (3, 1), (5, 0), (6, 0), (4, 1), (5, 1), (7, 0), (6, 1), (7, 1)) for x in range(2)]
     return {"t": t, "v": v, "s": s, "g": g, "q": q}
 
@@ -250,27 +250,14 @@ def tile_channelgroupattention_pa_kernel(tc, qkv_bn, gra_sharp, out_0, out_1):
             tiles["z%d" % s] = small.tile([P, P], F32, name="z%d" % (s % 2), tag="z%d" % (s % 2))
             return tiles["z%d" % s]
 
-        def red(s, k):
-            def emit(eng):
-                if k == 0:
-                    tiles["tf%d" % s] = small.tile([P, 2, P], F32, name="tf", tag="tf")
-                tf = tiles["tf%d" % s]
-                if k < 2:
-                    nc.vector.tensor_reduce(out=tf[:, k, :], in_=tiles["d%d" % s][:, 4 * k:4 * (k + 1), :].rearrange("p h c -> p c h"),
-                                            axis=AX.X, op=ALU.add)
-                else:
-                    nc.vector.tensor_reduce(out=new_z(s)[:], in_=tf[:].rearrange("p h c -> p c h"), axis=AX.X, op=ALU.add)
-            return emit
-
         def add(s, k):
             def emit(eng):
                 e = nc.gpsimd if eng == "g" else nc.vector
+                i, j = BLOCKS[s]
+                d = tiles["d%d" % s]
+                t1 = rng[j][:, i, 0:4, :]
                 if k == 0:
-                    tiles["t%d" % s] = small.tile([P, 4, P], F32, name="t1", tag="t1")
-                t1 = tiles["t%d" % s]
-                if k == 0:
-                    d = tiles["d%d" % s]
-                    e.tensor_tensor(out=t1[:], in0=d[:, 0:4, :], in1=d[:, 4:8, :], op=ALU.add)
+                    e.tensor_tensor(out=t1, in0=d[:, 0:4, :], in1=d[:, 4:8, :], op=ALU.add)
                 elif k == 1:
                     e.tensor_tensor(out=t1[:, 0:2, :], in0=t1[:, 0:2, :], in1=t1[:, 2:4, :], op=ALU.add)
                 else:
@@ -348,7 +335,7 @@ def tile_channelgroupattention_pa_kernel(tc, qkv_bn, gra_sharp, out_0, out_1):
             k = name[0]
             a = [int(ch) for ch in name[1:]]
             if k == "T":
-                idx = a[1] if a[0] == 0 else 6 + a[1] % 2
+                idx = a[1] if a[0] == 0 else 4 + a[1] % 4 if a[0] == 1 else 6 + a[1] % 2
                 ops[name] = ([freed[idx]] if idx in freed else [], transpose_x(name, a[0], a[1], idx))
                 ops["c" + name] = ([name], copy_x(name, a[0], a[1]))
                 freed[idx] = "c" + name
@@ -391,15 +378,13 @@ def tile_channelgroupattention_pa_kernel(tc, qkv_bn, gra_sharp, out_0, out_1):
             ops["E%d" % s] = (["B%d0" % s, "B%d1" % s], expo(s))
             zfree = ["R%d" % (s - 2)] if s >= 2 else []
             for k in range(3):
-                ops["F%d%d" % (s, k)] = (["E%d" % s] + (zfree + ["F%d0" % s, "F%d1" % s] if k == 2 else []), red(s, k))
                 for c in "DG":
                     ops["%s%d%d" % (c, s, k)] = ((["E%d" % s] if k == 0 else ["%s%d%d" % (c, s, k - 1)]) + (zfree if k == 2 else []), add(s, k))
-            last = [c for c in ("F%d2" % s, "D%d2" % s, "G%d2" % s) if c in where][0]
+            last = [c for c in ("D%d2" % s, "G%d2" % s) if c in where][0]
             ops["R%d" % s] = ([last] + (["U%d" % (s - 2)] if s >= 2 else []), recip(s))
             ops["U%d" % s] = (["R%d" % s], mult(s))
             ops["a%d" % s] = (["U%d" % s], store_attn(i, j))
             ops["b%d" % s] = (["cM%d0" % s, "cM%d1" % s], store_attn(j, i))
-        ops["D80"] = (["E8", "G72"], add(8, 0))
         for p in range(len(zord)):
             j, k = int(zord[p][0]), int(zord[p][1])
             need = ["Z" + zord[p - 4]] if p >= 4 else ["S37"]

from contextlib import ExitStack

import concourse.mybir as mybir
from concourse.masks import make_identity

F32 = mybir.dt.float32
BF16 = mybir.dt.bfloat16
U8 = mybir.dt.uint8
U32 = mybir.dt.uint32
FP8X4 = mybir.dt.float8_e4m3fn_x4
ALU = mybir.AluOpType
ACT = mybir.ActivationFunctionType
AX = mybir.AxisListType

P = 128
C = 512
H = 8
WD = 1024
T = C // P
KIB = 1024

FLOPS = 2 * 2 * H * C * C * WD


BLOCKS = [(0, 0), (1, 0), (2, 0), (3, 0), (1, 1), (2, 1), (3, 1), (2, 2), (3, 2), (3, 3)]
NB = len(BLOCKS)
LOADS = [(t, hp) for t in (0, 1) for hp in range(4)] + [(2, 0), (3, 0), (2, 1), (2, 2), (2, 3), (3, 1), (3, 2), (3, 3)]
GROUPS = [(0, 256), (2, 256)]
LATE = [6, 7, 2, 3, 6, 7, 2, 3]
ROTATE = [4, 5, 0, 1, 6, 7, 2, 3]
CODE_OFF = [0, 5, 10, 16, 21, 26, 32, 37]
H_OFF = [80, 84, 88, 92, 96, 100, 104, 108, 112, 116, 120, 124]
R4 = range(4)
R8 = range(8)


def soft(s):
    return ["A%d0" % s, "A%d1" % s, "X%d" % s, "B%d0" % s, "B%d1" % s]


def gsum(s):
    return ["G%d0" % s, "G%d1" % s, "G%d2" % s]


def tree(s):
    return ["D%d0" % s, "D%d1" % s, "D%d2" % s]


def ca(n, bs=R4):
    return ["cH%d0%d" % (n, b) for b in bs]


def cb(n, bs=(0, 2)):
    return ["cH%d1%d" % (n, b) for b in bs]


def scores(s):
    return ["S%d%d" % (s, n) for n in R8]


def programs():
    t = ['T00', 'T01']
    for n in (2, 4, 6):
        t += ['T0%d' % n, 'T0%d' % (n + 1), 'S0%d' % (n - 2), 'S0%d' % (n - 1)]
    t += ['T10', 'T11', 'S06', 'S07'] + ['T1%d' % n for n in range(2, 8)]
    for b, u in ((1, 2), (2, 3)):
        for n in (0, 2, 4, 6):
            t += ['S%d%d' % (b, n), 'S%d%d' % (b, n + 1), 'T%d%d' % (u, n), 'T%d%d' % (u, n + 1)]
    for b in (3, 4, 5):
        t += scores(b)
    t += ['M10', 'M11'] + scores(6) + ['M20', 'M21'] + scores(7) + ['M30', 'M31'] + scores(8) + ['M50', 'M51'] + scores(9)
    ha = [['H%d0%d' % (n, b) for b in R4] for n in R8]
    hb = [['H%d1%d' % (n, b) for b in R4] for n in R8]
    t += ha[0] + ha[1] + ha[2] + ['M60', 'M61'] + ha[3] + ['M80', 'M81'] + ha[4] + hb[0] + hb[1] + hb[2] + hb[3] + ha[5] + ha[6] + hb[4] + hb[5] + ha[7] + hb[6] + hb[7]
    v = ['cT01', 'cT03', 'cT05', 'cT07', 'A00', 'cT11', 'A01', 'cT13', 'X0', 'cT15', 'B00', 'B01', 'cT17', 'K2', 'A10', 'K3', 'A11', 'X1', 'B10', 'B11', 'Q0', 'cT33', 'A20', 'cT35', 'A21', 'R0', 'X2', 'cT37', 'B20', 'B21', 'Q1']
    vector_sums = [3]
    for b in (3, 4, 5):
        v += ['A%d0' % b] + (['R%d' % (b - 2)] if b - 2 not in vector_sums else []) + ['A%d1' % b, 'X%d' % b, 'B%d0' % b, 'B%d1' % b]
        if b - 1 in vector_sums:
            v += tree(b - 1) + ['R%d' % (b - 1)]
    v += ['A60', 'R4', 'Q2', 'A61', 'X6', 'B60', 'B61']
    v += ['D50', 'D60', 'D51', 'D61', 'D52', 'A70', 'R5', 'D62', 'A71', 'R6', 'X7', 'U6', 'B70', 'B71', 'Z00', 'Z01', 'A80', 'Z02', 'A81', 'Z03', 'X8', 'Z10', 'A90', 'B80', 'A91', 'B81', 'X9', 'R7', 'Z11', 'B90', 'B91']
    v += ['Q3', 'D80', 'D81', 'D82', 'D90', 'R8', 'D91', 'U8', 'D92', 'Z12', 'R9', 'U9', 'Q4', 'K10', 'Z13', 'K11', 'Z20', 'Z30', 'Q5']
    v += ['cH011', 'cH013', 'cH111', 'cH113', 'Z21', 'Z31', 'cH211', 'cH213', 'K12', 'cH311', 'cH313', 'K13', 'Q6', 'cH503', 'P22', 'K14', 'Z22', 'Z32', 'cH603', 'cH411', 'cH413', 'K15', 'Q7', 'cH511', 'cH513', 'P23', 'cH703', 'Z23', 'Z33', 'cH611', 'cH613', 'cH711', 'cH713']
    s = ['cT00', 'cT02', 'cT04', 'cT06', 'cT10', 'cT12', 'cT14', 'cT16', 'E0', 'cT20', 'cT21', 'cT22', 'cT23', 'cT24', 'cT25', 'cT26', 'cT27', 'cT30', 'cT31', 'E1', 'cT32', 'cT34', 'cT36', 'K4', 'E2']
    s += ['K5', 'E3', 'K6', 'E4', 'cM10', 'cM11', 'K7', 'E5', 'cM20', 'cM21', 'P00', 'E6', 'P01', 'P02', 'P03', 'cM30', 'cM31', 'K8', 'K9', 'cM50', 'cM51', 'P10', 'E7', 'P11']
    s += ca(0) + ['E8'] + ca(1) + ['E9', 'P12'] + ca(2) + ['P13', 'cM60', 'cM61'] + ca(3) + ['cM80', 'cM81', 'P30'] + ca(4) + ['P31'] + cb(0) + cb(1) + cb(2) + cb(3) + ['P32'] + ca(5, range(3)) + ca(6, range(3)) + ['P33'] + cb(4) + cb(5) + ca(7, range(3)) + cb(6) + cb(7)
    g = ['K0', 'K1'] + gsum(0) + gsum(1) + ['U0'] + gsum(2) + ['U1'] + ['U2'] + gsum(4) + ['U3'] + ['U4', 'U5'] + gsum(7) + ['U7', 'P20', 'P21']
    q = ["a0", "a1", "b1", "a2", "b2", "a3", "a4", "b3", "a5", "a6", "b5", "h000", "h001", "h100", "h101", "a7", "h200", "h201", "a8", "b6", "h300", "h301", "b8", "a9"]
    q += ["h%d%d%d" % (n, grp, x) for n, grp in ((4, 0), (0, 1), (1, 1), (2, 1), (3, 1), (5, 0), (6, 0), (4, 1), (5, 1), (7, 0), (6, 1), (7, 1)) for x in range(2)]
    return {"t": t, "v": v, "s": s, "g": g, "q": q}


def tile_channelgroupattention_pa_kernel(tc, qkv_bn, gra_sharp, out_0, out_1):
    nc = tc.nc
    x = qkv_bn.rearrange("b c w -> (b c) w")
    h2 = out_0.rearrange("b w c -> (b w) c")
    attn3 = out_1.rearrange("b n c d -> (b n) c d")

    with ExitStack() as ctx:
        big = ctx.enter_context(tc.tile_pool(name="big", bufs=1))
        const = ctx.enter_context(tc.tile_pool(name="const", bufs=1))
        small = ctx.enter_context(tc.tile_pool(name="small", bufs=1))
        stage = ctx.enter_context(tc.tile_pool(name="stage", bufs=1))
        psum = ctx.enter_context(tc.psum_pool(name="psum", bufs=1))
        ctx.enter_context(tc.manual_schedule())

        xs = [big.tile([P, T, 2 * WD], BF16, name="x%d" % hp, offset=hp * 16 * KIB, align_bytes=64) for hp in range(4)]
        qt = [big.tile([P, H, 4, P], F32, name="qt%d" % t, offset=(64 + 16 * t) * KIB, align_bytes=64) for t in range(T)]
        rng = [big.tile([P, T, H, P], F32, name="rng%d" % j, offset=(128 + 16 * j) * KIB, align_bytes=64) for j in range(T)]

        ident = const.tile([P, P], F32, name="ident")
        make_identity(nc, ident[:])
        g_bf = const.tile([P, 1], BF16, name="g_bf")
        with nc.allow_non_contiguous_dma(reason="one bf16 scalar to every partition"):
            nc.scalar.dma_start(out=g_bf[:], in_=gra_sharp.partition_broadcast(P))
        g_f = const.tile([P, 1], F32, name="g_f")
        nc.vector.tensor_copy(out=g_f[:], in_=g_bf[:])
        rg = const.tile([P, 1], F32, name="rg")
        nc.vector.reciprocal(out=rg[:], in_=g_f[:])
        asc = const.tile([P, H, C], U8, name="asc", align_bytes=64)

        for t, hp in LOADS:
            nc.sync.dma_start(out=xs[hp][:, t, :], in_=x[P * t:P * (t + 1), 2 * WD * hp:2 * WD * (hp + 1)])

        prog = programs()
        where = {}
        for e in prog:
            for name in prog[e]:
                where[name] = e
        tiles = {}
        ops = {}

        def bank(idx):
            return psum.tile([P, 4, P], F32, name="bk%d" % idx, tag="bk%d" % idx)

        def copy_on(eng, out, in_):
            if eng == "v":
                nc.vector.tensor_copy(out=out, in_=in_)
            else:
                nc.scalar.copy(out=out, in_=in_)

        def qtb(t, n, u, e):
            return qt[t][:, n, u, :].bitcast(BF16).rearrange("p (c e) -> p c e", e=2)[:, :, e]

        def transpose_x(name, t, n, idx):
            def emit(eng):
                tb = bank(idx)
                tiles[name] = tb
                base = WD * (n % 2)
                for u in range(4):
                    nc.tensor.transpose(tb[:, u, :], xs[n // 2][:, t, base + 256 * u:base + 256 * (u + 1)].bitcast(F32), ident[:])
            return emit

        def copy_x(name, t, n):
            def emit(eng):
                copy_on(eng, qt[t][:, n, :, :], tiles[name][:])
            return emit

        def score(s, n, idx):
            def emit(eng):
                i, j = BLOCKS[s]
                if n % 4 == 0:
                    tiles["sc%d%d" % (s, n // 4)] = bank(idx)
                for u in range(4):
                    for e in range(2):
                        nc.tensor.matmul(out=tiles["sc%d%d" % (s, n // 4)][:, n % 4, :], lhsT=qtb(i, n, u, e), rhs=qtb(j, n, u, e),
                                         start=(u == 0 and e == 0), stop=(u == 3 and e == 1))
            return emit

        def mirror(name, s, hh, idx):
            def emit(eng):
                i, j = BLOCKS[s]
                tb = bank(idx)
                tiles[name] = tb
                for nn in range(4):
                    nc.tensor.transpose(tb[:, nn, :], rng[j][:, i, 4 * hh + nn, :], ident[:])
            return emit

        def copy_mirror(name, s, hh):
            def emit(eng):
                i, j = BLOCKS[s]
                copy_on(eng, rng[i][:, j, 4 * hh:4 * (hh + 1), :], tiles[name][:])
            return emit

        def mx(name, n, grp, b, idx):
            def emit(eng):
                j0, width = GROUPS[grp]
                per = 512 // width
                bk = bank(idx)
                tiles[name] = bk
                flat = bk[:].rearrange("p a b -> p (a b)")
                codes, scales = tiles["q%d" % n]
                for q in range(per):
                    w8 = per * b + q
                    nc.tensor.matmul_mx(out=flat[:, width * q:width * (q + 1)],
                                        lhsT=codes[:, P * w8:P * (w8 + 1)].bitcast(FP8X4),
                                        lhsT_scale=scales[:, P * w8:P * (w8 + 1)],
                                        rhs=tiles["ac"][:, n, P * j0:P * j0 + width].bitcast(FP8X4),
                                        rhs_scale=asc[:, n, P * j0:P * j0 + width],
                                        start=True, stop=True)
            return emit

        def copy_h(name, key, slot, half):
            def emit(eng):
                if key not in tiles:
                    tiles[key] = big.tile([P, 2, 512], F32, name=key, offset=H_OFF[slot] * KIB, align_bytes=64)
                copy_on(eng, tiles[key][:, half, :], tiles[name][:].rearrange("p a b -> p (a b)"))
            return emit

        def store_h(key, n, grp, b):
            def emit(eng):
                j0, width = GROUPS[grp]
                per = 512 // width
                r0 = WD * n + P * per * b
                nc.sync.dma_start(out=h2[r0:r0 + 2 * per * P, P * j0:P * j0 + width].rearrange("(q p) c -> p q c", p=P),
                                  in_=tiles[key][:].rearrange("p x (y c) -> p (x y) c", c=width))
            return emit

        def smax(s, hh):
            def emit(eng):
                if hh == 0:
                    tiles["pm%d" % s] = small.tile([P, 2, P], F32, name="pm", tag="pm")
                nc.vector.tensor_reduce(out=tiles["pm%d" % s][:, hh, :], in_=tiles["sc%d%d" % (s, hh)][:].rearrange("p h c -> p c h"),
                                        axis=AX.X, op=ALU.max)
            return emit

        def smax2(s):
            def emit(eng):
                m = small.tile([P, P], F32, name="m%d" % (s % 2), tag="m%d" % (s % 2))
                tiles["m%d" % s] = m
                nc.vector.tensor_reduce(out=m[:], in_=tiles["pm%d" % s][:].rearrange("p h c -> p c h"), axis=AX.X, op=ALU.max)
            return emit

        def sub(s, hh, slot):
            def emit(eng):
                if hh == 0:
                    tiles["d%d" % s] = stage.tile([P, H, P], F32, name="d%d" % slot, tag="d%d" % slot)
                nc.vector.tensor_tensor(out=tiles["d%d" % s][:, 4 * hh:4 * (hh + 1), :], in0=tiles["sc%d%d" % (s, hh)][:],
                                        in1=tiles["m%d" % s][:].unsqueeze(1).to_broadcast([P, 4, P]), op=ALU.subtract)
            return emit

        def expo(s):
            def emit(eng):
                d = tiles["d%d" % s]
                nc.scalar.activation(out=d[:], in_=d[:], func=ACT.Exp, scale=rg[:, 0:1])
            return emit

        def new_z(s):
            tiles["z%d" % s] = small.tile([P, P], F32, name="z%d" % (s % 2), tag="z%d" % (s % 2))
            return tiles["z%d" % s]

        def add(s, k):
            def emit(eng):
                e = nc.gpsimd if eng == "g" else nc.vector
                i, j = BLOCKS[s]
                d = tiles["d%d" % s]
                t1 = rng[j][:, i, 0:4, :]
                if k == 0:
                    e.tensor_tensor(out=t1, in0=d[:, 0:4, :], in1=d[:, 4:8, :], op=ALU.add)
                elif k == 1:
                    e.tensor_tensor(out=t1[:, 0:2, :], in0=t1[:, 0:2, :], in1=t1[:, 2:4, :], op=ALU.add)
                else:
                    e.tensor_tensor(out=new_z(s)[:], in0=t1[:, 0, :], in1=t1[:, 1, :], op=ALU.add)
            return emit

        def recip(s):
            def emit(eng):
                r = small.tile([P, P], F32, name="r%d" % (s % 2), tag="r%d" % (s % 2))
                tiles["r%d" % s] = r
                nc.vector.reciprocal(out=r[:], in_=tiles["z%d" % s][:])
            return emit

        def mult(s):
            def emit(eng):
                i, j = BLOCKS[s]
                e = nc.gpsimd if eng == "g" else nc.vector
                e.tensor_tensor(out=rng[j][:, i, :, :], in0=tiles["d%d" % s][:],
                                in1=tiles["r%d" % s][:].unsqueeze(1).to_broadcast([P, H, P]), op=ALU.mult)
            return emit

        def store_attn(a, b):
            def emit(eng):
                nc.sync.dma_start(out=attn3[:, P * a:P * (a + 1), P * b:P * (b + 1)].rearrange("n p c -> p n c"), in_=rng[b][:, a, :, :])
            return emit

        def regroup_a(j, k, slot):
            def emit(eng):
                ga = stage.tile([P, 2, P, 4], BF16, name="ga%d" % slot, tag="ga%d" % slot, align_bytes=64)
                tiles["ga%d%d" % (j, k)] = ga
                src = rng[j][:, :, 2 * k:2 * (k + 1), :]
                if eng == "g":
                    nc.gpsimd.tensor_scalar(out=ga[:].rearrange("p n c t -> p (n c) t"), in0=src.rearrange("p t n c -> p (n c) t"),
                                            scalar1=1.0, scalar2=0.0, op0=ALU.mult, op1=ALU.add)
                else:
                    copy_on(eng, ga[:].rearrange("p n (q i) t -> p (n q) t i", i=4), src.rearrange("p t n (q i) -> p (n q) t i", i=4))
            return emit

        def quant_a(j, k):
            def emit(eng):
                if "ac" not in tiles:
                    tiles["ac"] = big.tile([P, H, C], U32, name="ac", offset=64 * KIB, align_bytes=64)
                for nn in range(2):
                    n = 2 * k + nn
                    nc.vector.quantize_mx(out=tiles["ac"][:, n, P * j:P * (j + 1)].bitcast(FP8X4), scales=asc[:, n, P * j:P * (j + 1)],
                                          in_=tiles["ga%d%d" % (j, k)][:, nn, :, :].rearrange("p c t -> p (c t)"))
            return emit

        def regroup_q(n, a):
            def emit(eng):
                key = "gq%d" % n
                if key not in tiles:
                    tiles[key] = stage.tile([P, WD, 4], BF16, name="gq%d" % (n % 2), tag="gq%d" % (n % 2), align_bytes=64)
                base = WD * (n % 2) + 512 * a
                src = xs[n // 2][:, :, base:base + 512]
                dst = tiles[key][:, 512 * a:512 * (a + 1), :]
                if eng == "g":
                    nc.gpsimd.tensor_scalar(out=dst, in0=src.rearrange("p t m -> p m t"), scalar1=1.0, scalar2=0.0, op0=ALU.mult, op1=ALU.add)
                else:
                    copy_on(eng, dst.rearrange("p (m i) t -> p m t i", i=4), src.rearrange("p t (m i) -> p m t i", i=4))
            return emit

        def quant_q(n):
            def emit(eng):
                codes = big.tile([P, WD], U32, name="qc%d" % n, offset=CODE_OFF[n] * KIB, align_bytes=64)
                scales = big.tile([P, WD], U8, name="qs%d" % n, offset=(CODE_OFF[n] + 4) * KIB, align_bytes=64)
                tiles["q%d" % n] = (codes, scales)
                nc.vector.quantize_mx(out=codes[:].bitcast(FP8X4), scales=scales[:], in_=tiles["gq%d" % n][:].rearrange("p w t -> p (w t)"))
            return emit

        freed = {}
        late = 0
        slots = {}
        for name in prog["t"]:
            k = name[0]
            a = [int(ch) for ch in name[1:]]
            if k == "T":
                idx = a[1] if a[0] == 0 else 4 + a[1] % 4 if a[0] == 1 else 6 + a[1] % 2
                ops[name] = ([freed[idx]] if idx in freed else [], transpose_x(name, a[0], a[1], idx))
                ops["c" + name] = ([name], copy_x(name, a[0], a[1]))
                freed[idx] = "c" + name
            elif k == "S":
                i, j = BLOCKS[a[0]]
                idx = 2 * (a[0] % 3) + a[1] // 4
                ops[name] = (["cT%d%d" % (i, a[1]), "cT%d%d" % (j, a[1])] + ([freed[idx]] if idx in freed else []), score(a[0], a[1], idx))
                if a[1] % 4 == 3:
                    freed[idx] = "B%d%d" % (a[0], a[1] // 4)
            elif k == "M":
                idx = 6 + a[1]
                ops[name] = (["U%d" % a[0], freed[idx]], mirror(name, a[0], a[1], idx))
                ops["c" + name] = ([name], copy_mirror(name, a[0], a[1]))
                freed[idx] = "c" + name
            else:
                n, grp, b = a
                idx = LATE[late] if late < len(LATE) else ROTATE[(late - len(LATE)) % 8]
                late += 1
                j0, width = GROUPS[grp]
                ops[name] = (["Q%d" % n, freed[idx]] + ["Z%d%d" % (j, n // 2) for j in range(j0, j0 + width // P)], mx(name, n, grp, b, idx))
                freed[idx] = "c" + name
                key = "h%d%d%d" % (n, grp, b // 2)
                if key not in slots:
                    slots[key] = len(slots)
                need = [name]
                if slots[key] >= len(H_OFF):
                    need.append([o for o in slots if slots[o] == slots[key] - len(H_OFF)][0])
                ops["c" + name] = (need, copy_h(name, key, slots[key] % len(H_OFF), b % 2))
                if b % 2 == 1:
                    ops[key] = (["cH%d%d%d" % (n, grp, b - 1), "cH%d%d%d" % (n, grp, b)], store_h(key, n, grp, b - 1))
        dord = [int(name[1]) for name in prog["v"] if name[0] == "B" and name[2] == "0"]
        zord = [name[1:] for name in prog["v"] if name[0] == "Z"]
        for s in range(NB):
            i, j = BLOCKS[s]
            for hh in range(2):
                ops["A%d%d" % (s, hh)] = (["S%d%d" % (s, 4 * hh + q) for q in range(4)], smax(s, hh))
                p = dord.index(s)
                ops["B%d%d" % (s, hh)] = (["X%d" % s] + (["U%d" % dord[p - 3]] if p >= 3 else []), sub(s, hh, p % 3))
            ops["X%d" % s] = (["A%d0" % s, "A%d1" % s], smax2(s))
            ops["E%d" % s] = (["B%d0" % s, "B%d1" % s], expo(s))
            zfree = ["R%d" % (s - 2)] if s >= 2 else []
            for k in range(3):
                for c in "DG":
                    ops["%s%d%d" % (c, s, k)] = ((["E%d" % s] if k == 0 else ["%s%d%d" % (c, s, k - 1)]) + (zfree if k == 2 else []), add(s, k))
            last = [c for c in ("D%d2" % s, "G%d2" % s) if c in where][0]
            ops["R%d" % s] = ([last] + (["U%d" % (s - 2)] if s >= 2 else []), recip(s))
            ops["U%d" % s] = (["R%d" % s], mult(s))
            ops["a%d" % s] = (["U%d" % s], store_attn(i, j))
            ops["b%d" % s] = (["cM%d0" % s, "cM%d1" % s], store_attn(j, i))
        for p in range(len(zord)):
            j, k = int(zord[p][0]), int(zord[p][1])
            need = ["Z" + zord[p - 4]] if p >= 4 else ["S37"]
            for i in range(T):
                if (i, j) in BLOCKS:
                    need.append("U%d" % BLOCKS.index((i, j)))
                else:
                    need.append("cM%d%d" % (BLOCKS.index((j, i)), k // 2))
            ops["P" + zord[p]] = (need, regroup_a(j, k, p % 4))
            ops["Z" + zord[p]] = (["P" + zord[p]], quant_a(j, k))
        for n in range(H):
            for a in range(2):
                ops["K%d" % (2 * n + a)] = (["Q%d" % (n - 2)] if n >= 2 else [], regroup_q(n, a))
            first = 0 if n < 3 else 4 if n < 6 else 8
            ops["Q%d" % n] = (["T3%d" % (first // 2), "T3%d" % (first // 2 + 1), "K%d" % (2 * n), "K%d" % (2 * n + 1)] + ["K%d" % q for q in range(first, first + 4)], quant_q(n))

        done = {}
        pos = {e: 0 for e in prog}
        total = len(where)
        while len(done) < total:
            before = len(done)
            for e in prog:
                while pos[e] < len(prog[e]) and all(o in done for o in ops[prog[e][pos[e]]][0]):
                    name = prog[e][pos[e]]
                    ops[name][1](e)
                    done[name] = True
                    pos[e] += 1
            assert len(done) > before, ["%s" % prog[e][pos[e]] for e in prog if pos[e] < len(prog[e])]
